import numpy as np
import ml_dtypes


def mxq(x, axis, fmt="e4m3"):
    dtype, down = {"e4m3": (ml_dtypes.float8_e4m3fn, 7), "e5m2": (ml_dtypes.float8_e5m2, 14)}[fmt]
    v = np.moveaxis(np.asarray(x, np.float32).astype(ml_dtypes.bfloat16).astype(np.float64), axis, -1)
    blocks = v.reshape(v.shape[:-1] + (-1, 32))
    amax = np.abs(blocks).max(-1, keepdims=True)
    byte = np.maximum(np.where(amax > 0, np.frexp(amax)[1] - 1 + 127, 0) - down, 1)
    scale = np.exp2(byte - 127.0)
    codes = (blocks / scale).astype(np.float32).astype(dtype).astype(np.float64)
    return np.moveaxis((codes * scale).reshape(v.shape), -1, axis)


WIDE = False


def mx_kscale(k):
    if not WIDE:
        return np.ones(k)
    levels = np.array([10, -10, 5, -5, 0])
    if k % 512:
        return np.exp2(np.random.permutation(np.resize(levels, k // 32))).repeat(32)
    a = np.empty((k // 512, 16))
    for p in range(k // 512):
        a[p, :8] = np.random.permutation(np.resize(levels, 8))
        for g in range(8):
            far = levels[np.abs(levels - a[p, g]) >= 10]
            a[p, g + 8] = far[np.random.randint(len(far))]
    return np.exp2(a.ravel()).repeat(32)


BF16 = ml_dtypes.bfloat16


def bf(x):
    return np.asarray(x, np.float32).astype(BF16)


def f64(x):
    return np.asarray(x).astype(np.float64)


B, T, D, NH, N_MLP = 4, 1024, 512, 16, 512
LN_EPS = 1e-6


def layer_norm(v, g, b):
    mu = v.mean(-1, keepdims=True)
    var = np.square(v - mu).mean(-1, keepdims=True)
    return (v - mu) / np.sqrt(var + LN_EPS) * g + b


def erf(v):
    z = np.clip(v, -6.0, 6.0)
    r = 2.0 * z * z
    term = z.copy()
    total = z.copy()
    for n in range(1, 120):
        term = term * r / (2.0 * n + 1.0)
        total = total + term
    return 2.0 / np.sqrt(np.pi) * np.exp(-z * z) * total


def gelu_erf(v):
    return 0.5 * v * (1.0 + erf(v / np.sqrt(2.0)))


def setup_inputs():
    s, t = mx_kscale(D), mx_kscale(D)
    return {"attn_out": bf(np.random.standard_normal((B, T, D)) * 0.25 * s),
            "x": bf(np.random.standard_normal((B, T, D)) * 1.5 + np.random.standard_normal((B, T, 1)) * 0.5),
            "W_proj": bf(np.random.standard_normal((D, D)) * 3.0 / np.sqrt(D) / s),
            "b_proj": bf(np.random.standard_normal(D) * 0.2),
            "g2": bf((1.0 + 0.1 * np.random.standard_normal(D)) * t),
            "beta2": bf(0.1 * np.random.standard_normal(D) * t),
            "W1": bf(np.random.standard_normal((N_MLP, D)) / np.sqrt(D) / t),
            "b1": bf(np.random.standard_normal(N_MLP) * 0.2)}


def reference(attn_out, x, W_proj, b_proj, g2, beta2, W1, b1):
    o = (mxq(f64(attn_out), 2, "e4m3") @ mxq(f64(W_proj), 1, "e4m3").T) + f64(b_proj)
    x_mid = f64(x) + o
    h = layer_norm(x_mid, f64(g2), f64(beta2))
    u = gelu_erf((mxq(h, 2, "e4m3") @ mxq(f64(W1), 1, "e4m3").T) + f64(b1))
    return x_mid, u

@@ -1,0 +1,359 @@
+from contextlib import ExitStack
+
+import concourse.mybir as mybir
+from concourse.masks import make_identity
+
+F32 = mybir.dt.float32
+BF16 = mybir.dt.bfloat16
+U32 = mybir.dt.uint32
+U8 = mybir.dt.uint8
+FP8X4 = mybir.dt.float8_e4m3fn_x4
+ALU = mybir.AluOpType
+ACT = mybir.ActivationFunctionType
+
+P = 128
+RUN = 8
+PACK = 4
+D = P * PACK
+TOKENS = 4 * 1024
+GROUP_TILES = 4
+GROUP_TOKENS = GROUP_TILES * P
+HALF = GROUP_TOKENS // 2
+GROUPS = TOKENS // GROUP_TOKENS
+STAT_COLS = GROUPS * GROUP_TILES
+LN_EPS = 1e-6
+
+FLOPS = 2 * 2 * TOKENS * D * D
+
+
+def tile_block_pb_t_kernel(tc, attn_out, x, W_proj, b_proj, g2, beta2, W1, b1, out_0, out_1):
+    nc = tc.nc
+
+    def by_group(rows):
+        return rows.flatten_outer_dims().rearrange("(g p j) d -> g p j d", p=P, j=GROUP_TILES)
+
+    attn_groups, x_groups = by_group(attn_out), by_group(x)
+    x_mid_groups, u_groups = by_group(out_0), by_group(out_1)
+
+    with ExitStack() as ctx:
+        const = ctx.enter_context(tc.tile_pool(name="const", bufs=1))
+        resident = ctx.enter_context(tc.tile_pool(name="resident", bufs=1))
+        inputs = ctx.enter_context(tc.tile_pool(name="inputs", bufs=4))
+        pairs = ctx.enter_context(tc.tile_pool(name="pairs", bufs=2))
+        triples = ctx.enter_context(tc.tile_pool(name="triples", bufs=3))
+        flipped = ctx.enter_context(tc.psum_pool(name="flipped", bufs=4))
+        sums = ctx.enter_context(tc.psum_pool(name="sums", bufs=4))
+
+        attn_rows, x_rows = {}, {}
+
+        def load(g):
+            if not 0 <= g < GROUPS:
+                return
+            attn_rows[g] = inputs.tile([P, GROUP_TILES, D], BF16, name="attn_rows")
+            nc.sync.dma_start(out=attn_rows[g][:], in_=attn_groups[g])
+            x_rows[g] = inputs.tile([P, GROUP_TILES, D], BF16, name="x_rows")
+            nc.sync.dma_start(out=x_rows[g][:], in_=x_groups[g])
+
+        bias_rows = const.tile([P, 2, D], BF16)
+        nc.vector.memset(bias_rows[:], 0.0)
+        ln_rows = const.tile([P, P], BF16)
+        nc.vector.memset(ln_rows[:], 0.0)
+        nc.sync.dma_start(out=bias_rows[0:1, 0, :], in_=b_proj.rearrange("(o d) -> o d", o=1))
+        nc.sync.dma_start(out=bias_rows[0:1, 1, :], in_=b1.rearrange("(o d) -> o d", o=1))
+        nc.sync.dma_start(out=ln_rows[0:PACK, :].rearrange("t (q r) -> t q r", r=RUN), in_=g2.rearrange("(q t r) -> t q r", t=PACK, r=RUN))
+        nc.sync.dma_start(out=ln_rows[PACK : 2 * PACK, :].rearrange("t (q r) -> t q r", r=RUN), in_=beta2.rearrange("(q t r) -> t q r", t=PACK, r=RUN))
+
+        wp_rows = const.tile([P, PACK, D], BF16)
+        nc.sync.dma_start(out=wp_rows[:], in_=W_proj.rearrange("(c p) k -> p c k", p=P))
+        load(0)
+        load(1)
+        load(2)
+        w1_rows = const.tile([P, PACK, D], BF16)
+        nc.sync.dma_start(out=w1_rows[:], in_=W1.rearrange("(c p) k -> p c k", p=P))
+
+        warm = const.tile([P, 1], F32)
+        nc.vector.memset(warm[:], 0.0)
+        nc.scalar.activation(out=warm[:], in_=warm[:], func=ACT.Gelu)
+
+        ident_f32 = const.tile([P, P], F32)
+        make_identity(nc, ident_f32[:])
+        ident_bf16 = const.tile([P, P], BF16)
+        make_identity(nc, ident_bf16[:])
+        ones = const.tile([P, P], BF16)
+        nc.vector.memset(ones[:], 1.0)
+        neg_half = const.tile([P, GROUP_TILES], F32)
+        nc.vector.memset(neg_half[:], -0.5)
+
+        row_sum = const.tile([P, STAT_COLS], F32)
+        neg_mean = const.tile([P, STAT_COLS], F32)
+        sq_sum = const.tile([P, STAT_COLS], F32)
+        var_eps = const.tile([P, STAT_COLS], F32)
+        rstd = const.tile([P, STAT_COLS], F32)
+
+        def stat_cols(g):
+            return slice(g * GROUP_TILES, (g + 1) * GROUP_TILES)
+
+        def stat_col(g, j):
+            return slice(g * GROUP_TILES + j, g * GROUP_TILES + j + 1)
+
+        bias_bcast = const.tile([P, 2, D], F32)
+        for i in range(2):
+            spread = sums.tile([P, D], F32, name="acc")
+            nc.tensor.matmul(out=spread[:], lhsT=ones[:], rhs=bias_rows[:, i, :], start=True, stop=True)
+            nc.scalar.copy(out=bias_bcast[:, i, :], in_=spread[:])
+
+        ln_flipped = flipped.tile([P, P], BF16, name="bank")
+        nc.tensor.transpose(ln_flipped[:], ln_rows[:], ident_bf16[:])
+        ln_cols = const.tile([P, 2 * PACK], F32)
+        nc.scalar.copy(out=ln_cols[:], in_=ln_flipped[:, 0 : 2 * PACK])
+
+        def flip_words(rows):
+            row_words = rows.bitcast(F32)
+            banks = []
+            for half in range(2):
+                bank = flipped.tile([P, 2, HALF], F32, name="bank")
+                for jj in range(2):
+                    for u in range(2):
+                        nc.tensor.transpose(
+                            bank[:, u, jj * P : (jj + 1) * P],
+                            row_words[:, 2 * half + jj, u : 2 * P : 2],
+                            ident_f32[:],
+                        )
+                banks.append(bank)
+            return banks
+
+        def copy_words(banks, grouped):
+            grouped_words = grouped.bitcast(F32)
+            for half in range(2):
+                nc.scalar.copy(
+                    out=grouped_words[:, half * HALF : (half + 1) * HALF, :],
+                    in_=banks[half][:].rearrange("p u w -> p w u"),
+                )
+
+        def quantise(grouped, operand):
+            codes, scales = operand
+            nc.vector.quantize_mx(
+                out=codes[:].bitcast(FP8X4), scales=scales[:], in_=grouped.rearrange("p w t -> p (w t)")
+            )
+
+        def mx_operand(pool, name):
+            codes = pool.tile([P, GROUP_TOKENS], U32, name=name + "_codes", align_bytes=64)
+            scales = pool.tile([P, GROUP_TOKENS], U8, name=name + "_scales", align_bytes=64)
+            return codes, scales
+
+        def matmul_mx_tile(acc, tokens_operand, j, weight_operand):
+            tokens = slice(j * P, (j + 1) * P)
+            nc.tensor.matmul_mx(
+                out=acc[:],
+                lhsT=tokens_operand[0][:, tokens].bitcast(FP8X4),
+                lhsT_scale=tokens_operand[1][:, tokens],
+                rhs=weight_operand[0][:].bitcast(FP8X4),
+                rhs_scale=weight_operand[1][:],
+                start=True,
+                stop=True,
+            )
+
+        wp_grouped = pairs.tile([P, D, PACK], BF16, name="a_grouped", align_bytes=64)
+        copy_words(flip_words(wp_rows[:]), wp_grouped[:])
+        wp_operand = mx_operand(const, "wp")
+        quantise(wp_grouped[:], wp_operand)
+
+        w1_operand = mx_operand(const, "w1")
+        w1_grouped = const.tile([P, D, PACK], BF16, align_bytes=64)
+        w1_ordered = const.tile([P, PACK, D], BF16)
+
+        def order_w1():
+            for c in range(PACK):
+                nc.vector.tensor_copy(
+                    out=w1_ordered[:, c, :].rearrange("p (t q r) -> p t q r", t=PACK, r=RUN),
+                    in_=w1_rows[:, c, :].rearrange("p (q t r) -> p t q r", t=PACK, r=RUN),
+                )
+
+        def flip_w1():
+            for half in range(2):
+                bank = flipped.tile([P, PACK, HALF], BF16, name="bank")
+                for cc in range(2):
+                    for t in range(PACK):
+                        nc.tensor.transpose(
+                            bank[:, t, cc * P : (cc + 1) * P],
+                            w1_ordered[:, 2 * half + cc, t * P : (t + 1) * P],
+                            ident_bf16[:],
+                        )
+                nc.scalar.copy(
+                    out=w1_grouped[:, half * HALF : (half + 1) * HALF, :],
+                    in_=bank[:].rearrange("p t n -> p n t"),
+                )
+
+        a_banks, a_grouped, a_operand, x_mid = {}, {}, {}, {}
+        normed, h_banks, h_planes, h_grouped, h_operand, hidden = {}, {}, {}, {}, {}, {}
+
+        def add_bias(g):
+            if not 0 <= g < GROUPS:
+                return
+            x_mid[g] = resident.tile([P, GROUP_TILES, D], F32, name="x_mid_%d" % g)
+            nc.vector.tensor_tensor(
+                out=x_mid[g][:],
+                in0=x_rows[g][:],
+                in1=bias_bcast[:, 0:1, :].to_broadcast([P, GROUP_TILES, D]),
+                op=ALU.add,
+            )
+
+        def flip_attention(g):
+            if not 0 <= g < GROUPS:
+                return
+            a_banks[g] = flip_words(attn_rows[g][:])
+
+        def copy_attention(g):
+            if not 0 <= g < GROUPS:
+                return
+            a_grouped[g] = pairs.tile([P, GROUP_TOKENS, PACK], BF16, name="a_grouped", align_bytes=64)
+            copy_words(a_banks[g], a_grouped[g][:])
+
+        def quantise_attention(g):
+            if not 0 <= g < GROUPS:
+                return
+            a_operand[g] = mx_operand(triples, "a")
+            quantise(a_grouped[g][:], a_operand[g])
+
+        def project_attention(g):
+            if not 0 <= g < GROUPS:
+                return
+            for j in range(GROUP_TILES):
+                acc = sums.tile([P, D], F32, name="acc")
+                matmul_mx_tile(acc, a_operand[g], j, wp_operand)
+                nc.vector.scalar_tensor_tensor(
+                    out=x_mid[g][:, j, :],
+                    in0=acc[:],
+                    scalar=1.0,
+                    in1=x_mid[g][:, j, :],
+                    op0=ALU.mult,
+                    op1=ALU.add,
+                    accum_out=row_sum[:, stat_col(g, j)],
+                )
+
+        def variance(g):
+            if not 0 <= g < GROUPS:
+                return
+            nc.scalar.mul(out=neg_mean[:, stat_cols(g)], in_=row_sum[:, stat_cols(g)], mul=-1.0 / D)
+            squares = pairs.tile([P, GROUP_TILES, D], BF16, name="squares")
+            for j in range(GROUP_TILES):
+                nc.scalar.activation(
+                    out=squares[:, j, :],
+                    in_=x_mid[g][:, j, :],
+                    func=ACT.Square,
+                    bias=neg_mean[:, stat_col(g, j)],
+                    scale=1.0,
+                    accum_out=sq_sum[:, stat_col(g, j)],
+                )
+            nc.sync.dma_start(out=x_mid_groups[g], in_=x_mid[g][:])
+
+        def reciprocal_std(g):
+            if not 0 <= g < GROUPS:
+                return
+            nc.gpsimd.tensor_scalar(
+                out=var_eps[:, stat_cols(g)],
+                in0=sq_sum[:, stat_cols(g)],
+                scalar1=1.0 / D,
+                scalar2=LN_EPS,
+                op0=ALU.mult,
+                op1=ALU.add,
+            )
+            nc.gpsimd.tensor_tensor(
+                out=rstd[:, stat_cols(g)], in0=var_eps[:, stat_cols(g)], in1=neg_half[:], op=ALU.pow
+            )
+
+        def normalise(g):
+            if not 0 <= g < GROUPS:
+                return
+            normed[g] = pairs.tile([P, GROUP_TILES, D], F32, name="normed")
+            for j in range(GROUP_TILES):
+                nc.vector.tensor_scalar(
+                    out=normed[g][:, j, :].rearrange("p (t q r) -> p t q r", t=PACK, r=RUN),
+                    in0=x_mid[g][:, j, :].rearrange("p (q t r) -> p t q r", t=PACK, r=RUN),
+                    scalar1=neg_mean[:, stat_col(g, j)],
+                    scalar2=rstd[:, stat_col(g, j)],
+                    op0=ALU.add,
+                    op1=ALU.mult,
+                )
+
+        def flip_normed(g):
+            if not 0 <= g < GROUPS:
+                return
+            h_banks[g] = []
+            for t in range(PACK):
+                bank = flipped.tile([P, GROUP_TOKENS], F32, name="bank")
+                for j in range(GROUP_TILES):
+                    nc.tensor.transpose(
+                        bank[:, j * P : (j + 1) * P], normed[g][:, j, t * P : (t + 1) * P], ident_f32[:]
+                    )
+                h_banks[g].append(bank)
+
+        def scale_shift(g):
+            if not 0 <= g < GROUPS:
+                return
+            h_planes[g] = pairs.tile([P, PACK, GROUP_TOKENS], BF16, name="h_planes")
+            for t in range(PACK):
+                nc.scalar.activation(
+                    out=h_planes[g][:, t, :],
+                    in_=h_banks[g][t][:],
+                    func=ACT.Identity,
+                    scale=ln_cols[:, t : t + 1],
+                    bias=ln_cols[:, PACK + t : PACK + t + 1],
+                )
+
+        def regroup_h(g):
+            if not 0 <= g < GROUPS:
+                return
+            h_grouped[g] = pairs.tile([P, GROUP_TOKENS, PACK], BF16, name="h_grouped", align_bytes=64)
+            nc.vector.tensor_copy(
+                out=h_grouped[g][:].rearrange("p (c i) t -> p c t i", i=4),
+                in_=h_planes[g][:].rearrange("p t (c i) -> p c t i", i=4),
+            )
+
+        def quantise_h(g):
+            if not 0 <= g < GROUPS:
+                return
+            h_operand[g] = mx_operand(triples, "h")
+            quantise(h_grouped[g][:], h_operand[g])
+
+        def project_h(g):
+            if not 0 <= g < GROUPS:
+                return
+            hidden[g] = triples.tile([P, GROUP_TILES, D], F32, name="hidden")
+            for j in range(GROUP_TILES):
+                acc = sums.tile([P, D], F32, name="acc")
+                matmul_mx_tile(acc, h_operand[g], j, w1_operand)
+                nc.vector.tensor_tensor(
+                    out=hidden[g][:, j, :], in0=acc[:], in1=bias_bcast[:, 1, :], op=ALU.add
+                )
+
+        def gelu(g):
+            if not 0 <= g < GROUPS:
+                return
+            for j in range(GROUP_TILES):
+                nc.scalar.activation(out=hidden[g][:, j, :], in_=hidden[g][:, j, :], func=ACT.Gelu)
+                nc.sync.dma_start(out=u_groups[g][:, j, :], in_=hidden[g][:, j, :])
+
+        W1_STEP = 2
+        for step in range(-3, GROUPS + 5):
+            project_attention(step)
+            normalise(step - 1)
+            project_h(step - 5)
+            scale_shift(step - 2)
+            copy_attention(step + 2)
+            if step == W1_STEP - 1:
+                order_w1()
+            if step == W1_STEP:
+                flip_w1()
+            variance(step)
+            quantise_h(step - 3)
+            quantise_attention(step + 2)
+            if step == W1_STEP + 1:
+                quantise(w1_grouped[:], w1_operand)
+            flip_normed(step - 1)
+            gelu(step - 5)
+            add_bias(step + 3)
+            flip_attention(step + 3)
+            reciprocal_std(step)
+            regroup_h(step - 2)
+            load(step + 6)

@@ -42,7 +42,8 @@ def tile_block_pb_t_kernel(tc, attn_out, x, W_proj, b_proj, g2, beta2, W1, b1, o
         pairs = ctx.enter_context(tc.tile_pool(name="pairs", bufs=2))
         triples = ctx.enter_context(tc.tile_pool(name="triples", bufs=3))
         flipped = ctx.enter_context(tc.psum_pool(name="flipped", bufs=4))
-        sums = ctx.enter_context(tc.psum_pool(name="sums", bufs=4))
+        sums = ctx.enter_context(tc.psum_pool(name="sums", bufs=3))
+        held = ctx.enter_context(tc.psum_pool(name="held", bufs=1))
 
         attn_rows, x_rows = {}, {}
 
@@ -96,11 +97,12 @@ def tile_block_pb_t_kernel(tc, attn_out, x, W_proj, b_proj, g2, beta2, W1, b1, o
         def stat_col(g, j):
             return slice(g * GROUP_TILES + j, g * GROUP_TILES + j + 1)
 
-        bias_bcast = const.tile([P, 2, D], F32)
-        for i in range(2):
-            spread = sums.tile([P, D], F32, name="acc")
-            nc.tensor.matmul(out=spread[:], lhsT=ones[:], rhs=bias_rows[:, i, :], start=True, stop=True)
-            nc.scalar.copy(out=bias_bcast[:, i, :], in_=spread[:])
+        b_proj_bcast = held.tile([P, 1, D], F32)
+        nc.tensor.matmul(out=b_proj_bcast[:, 0, :], lhsT=ones[:], rhs=bias_rows[:, 0, :], start=True, stop=True)
+        b1_bcast = const.tile([P, D], F32)
+        spread = sums.tile([P, D], F32, name="acc")
+        nc.tensor.matmul(out=spread[:], lhsT=ones[:], rhs=bias_rows[:, 1, :], start=True, stop=True)
+        nc.scalar.copy(out=b1_bcast[:], in_=spread[:])
 
         ln_flipped = flipped.tile([P, P], BF16, name="bank")
         nc.tensor.transpose(ln_flipped[:], ln_rows[:], ident_bf16[:])
@@ -194,7 +196,7 @@ def tile_block_pb_t_kernel(tc, attn_out, x, W_proj, b_proj, g2, beta2, W1, b1, o
             nc.vector.tensor_tensor(
                 out=x_mid[g][:],
                 in0=x_rows[g][:],
-                in1=bias_bcast[:, 0:1, :].to_broadcast([P, GROUP_TILES, D]),
+                in1=b_proj_bcast[:].to_broadcast([P, GROUP_TILES, D]),
                 op=ALU.add,
             )
 
@@ -267,7 +269,7 @@ def tile_block_pb_t_kernel(tc, attn_out, x, W_proj, b_proj, g2, beta2, W1, b1, o
                 return
             normed[g] = pairs.tile([P, GROUP_TILES, D], F32, name="normed")
             for j in range(GROUP_TILES):
-                nc.vector.tensor_scalar(
+                nc.gpsimd.tensor_scalar(
                     out=normed[g][:, j, :].rearrange("p (t q r) -> p t q r", t=PACK, r=RUN),
                     in0=x_mid[g][:, j, :].rearrange("p (q t r) -> p t q r", t=PACK, r=RUN),
                     scalar1=neg_mean[:, stat_col(g, j)],
@@ -324,7 +326,7 @@ def tile_block_pb_t_kernel(tc, attn_out, x, W_proj, b_proj, g2, beta2, W1, b1, o
                 acc = sums.tile([P, D], F32, name="acc")
                 matmul_mx_tile(acc, h_operand[g], j, w1_operand)
                 nc.vector.tensor_tensor(
-                    out=hidden[g][:, j, :], in0=acc[:], in1=bias_bcast[:, 1, :], op=ALU.add
+                    out=hidden[g][:, j, :], in0=acc[:], in1=b1_bcast[:], op=ALU.add
                 )
 
         def gelu(g):

@@ -16,12 +16,18 @@ RUN = 8
 PACK = 4
 D = P * PACK
 TOKENS = 4 * 1024
-GROUP_TILES = 4
-GROUP_TOKENS = GROUP_TILES * P
-HALF = GROUP_TOKENS // 2
-GROUPS = TOKENS // GROUP_TOKENS
-STAT_COLS = GROUPS * GROUP_TILES
+BATCH_TILES = 4
+BATCHES = TOKENS // (BATCH_TILES * P)
+WIDEST = BATCH_TILES * P
+STAT_COLS = BATCHES * BATCH_TILES
 LN_EPS = 1e-6
+
+SMALL = BATCH_TILES // 2
+GROUPS = (
+    [(0, 0, SMALL), (0, SMALL, SMALL)]
+    + [(b, 0, BATCH_TILES) for b in range(1, BATCHES - 1)]
+    + [(BATCHES - 1, 0, SMALL), (BATCHES - 1, SMALL, SMALL)]
+)
 
 FLOPS = 2 * 2 * TOKENS * D * D
 
@@ -29,48 +35,61 @@ FLOPS = 2 * 2 * TOKENS * D * D
 def tile_block_pb_t_kernel(tc, attn_out, x, W_proj, b_proj, g2, beta2, W1, b1, out_0, out_1):
     nc = tc.nc
 
-    def by_group(rows):
-        return rows.flatten_outer_dims().rearrange("(g p j) d -> g p j d", p=P, j=GROUP_TILES)
+    def by_batch(rows):
+        return rows.flatten_outer_dims().rearrange("(b p j) d -> b p j d", p=P, j=BATCH_TILES)
 
-    attn_groups, x_groups = by_group(attn_out), by_group(x)
-    x_mid_groups, u_groups = by_group(out_0), by_group(out_1)
+    attn_batches, x_batches = by_batch(attn_out), by_batch(x)
+    x_mid_batches, u_batches = by_batch(out_0), by_batch(out_1)
 
     with ExitStack() as ctx:
         const = ctx.enter_context(tc.tile_pool(name="const", bufs=1))
-        resident = ctx.enter_context(tc.tile_pool(name="resident", bufs=1))
-        inputs = ctx.enter_context(tc.tile_pool(name="inputs", bufs=4))
+        inputs = ctx.enter_context(tc.tile_pool(name="inputs", bufs=BATCHES))
         pairs = ctx.enter_context(tc.tile_pool(name="pairs", bufs=2))
         triples = ctx.enter_context(tc.tile_pool(name="triples", bufs=3))
+        sixes = ctx.enter_context(tc.tile_pool(name="sixes", bufs=6))
         flipped = ctx.enter_context(tc.psum_pool(name="flipped", bufs=4))
         sums = ctx.enter_context(tc.psum_pool(name="sums", bufs=3))
         held = ctx.enter_context(tc.psum_pool(name="held", bufs=1))
 
         attn_rows, x_rows = {}, {}
 
-        def load(g):
-            if not 0 <= g < GROUPS:
-                return
-            attn_rows[g] = inputs.tile([P, GROUP_TILES, D], BF16, name="attn_rows")
-            nc.sync.dma_start(out=attn_rows[g][:], in_=attn_groups[g])
-            x_rows[g] = inputs.tile([P, GROUP_TILES, D], BF16, name="x_rows")
-            nc.sync.dma_start(out=x_rows[g][:], in_=x_groups[g])
+        def load_attn(b, tiles):
+            nc.sync.dma_start(out=attn_rows[b][:, tiles, :], in_=attn_batches[b][:, tiles, :])
 
+        def load_x(b, tiles):
+            nc.sync.dma_start(out=x_rows[b][:, tiles, :], in_=x_batches[b][:, tiles, :])
+
+        for b in range(BATCHES):
+            attn_rows[b] = inputs.tile([P, BATCH_TILES, D], BF16, name="attn_rows")
+            x_rows[b] = inputs.tile([P, BATCH_TILES, D], BF16, name="x_rows")
+
+        early = slice(0, SMALL)
+        late = slice(SMALL, BATCH_TILES)
+        whole = slice(0, BATCH_TILES)
         bias_rows = const.tile([P, 2, D], BF16)
-        nc.vector.memset(bias_rows[:], 0.0)
-        ln_rows = const.tile([P, P], BF16)
-        nc.vector.memset(ln_rows[:], 0.0)
+        nc.vector.memset(bias_rows[:, 0, :], 0.0)
+        load_x(0, whole)
         nc.sync.dma_start(out=bias_rows[0:1, 0, :], in_=b_proj.rearrange("(o d) -> o d", o=1))
-        nc.sync.dma_start(out=bias_rows[0:1, 1, :], in_=b1.rearrange("(o d) -> o d", o=1))
-        nc.sync.dma_start(out=ln_rows[0:PACK, :].rearrange("t (q r) -> t q r", r=RUN), in_=g2.rearrange("(q t r) -> t q r", t=PACK, r=RUN))
-        nc.sync.dma_start(out=ln_rows[PACK : 2 * PACK, :].rearrange("t (q r) -> t q r", r=RUN), in_=beta2.rearrange("(q t r) -> t q r", t=PACK, r=RUN))
-
         wp_rows = const.tile([P, PACK, D], BF16)
         nc.sync.dma_start(out=wp_rows[:], in_=W_proj.rearrange("(c p) k -> p c k", p=P))
-        load(0)
-        load(1)
-        load(2)
+        load_attn(0, early)
+        load_attn(0, late)
+        load_x(1, whole)
+        nc.vector.memset(bias_rows[:, 1, :], 0.0)
+        ln_rows = const.tile([P, P], BF16)
+        nc.vector.memset(ln_rows[:], 0.0)
+        nc.sync.dma_start(out=bias_rows[0:1, 1, :], in_=b1.rearrange("(o d) -> o d", o=1))
+        for i, vec in enumerate((g2, beta2)):
+            nc.sync.dma_start(
+                out=ln_rows[i * PACK : (i + 1) * PACK, :].rearrange("t (q r) -> t q r", r=RUN),
+                in_=vec.rearrange("(q t r) -> t q r", t=PACK, r=RUN),
+            )
+        load_attn(1, whole)
         w1_rows = const.tile([P, PACK, D], BF16)
         nc.sync.dma_start(out=w1_rows[:], in_=W1.rearrange("(c p) k -> p c k", p=P))
+        for b in range(2, BATCHES):
+            load_x(b, whole)
+            load_attn(b, whole)
 
         warm = const.tile([P, 1], F32)
         nc.vector.memset(warm[:], 0.0)
@@ -82,7 +101,7 @@ def tile_block_pb_t_kernel(tc, attn_out, x, W_proj, b_proj, g2, beta2, W1, b1, o
         make_identity(nc, ident_bf16[:])
         ones = const.tile([P, P], BF16)
         nc.vector.memset(ones[:], 1.0)
-        neg_half = const.tile([P, GROUP_TILES], F32)
+        neg_half = const.tile([P, BATCH_TILES], F32)
         nc.vector.memset(neg_half[:], -0.5)
 
         row_sum = const.tile([P, STAT_COLS], F32)
@@ -91,29 +110,29 @@ def tile_block_pb_t_kernel(tc, attn_out, x, W_proj, b_proj, g2, beta2, W1, b1, o
         var_eps = const.tile([P, STAT_COLS], F32)
         rstd = const.tile([P, STAT_COLS], F32)
 
+        def width(g):
+            return GROUPS[g][2] * P
+
+        def tiles_of(g):
+            return range(GROUPS[g][2])
+
+        def batch_tiles(g):
+            b, first, count = GROUPS[g]
+            return b, slice(first, first + count)
+
         def stat_cols(g):
-            return slice(g * GROUP_TILES, (g + 1) * GROUP_TILES)
+            b, first, count = GROUPS[g]
+            return slice(b * BATCH_TILES + first, b * BATCH_TILES + first + count)
 
         def stat_col(g, j):
-            return slice(g * GROUP_TILES + j, g * GROUP_TILES + j + 1)
-
-        b_proj_bcast = held.tile([P, 1, D], F32)
-        nc.tensor.matmul(out=b_proj_bcast[:, 0, :], lhsT=ones[:], rhs=bias_rows[:, 0, :], start=True, stop=True)
-        b1_bcast = const.tile([P, D], F32)
-        spread = sums.tile([P, D], F32, name="acc")
-        nc.tensor.matmul(out=spread[:], lhsT=ones[:], rhs=bias_rows[:, 1, :], start=True, stop=True)
-        nc.scalar.copy(out=b1_bcast[:], in_=spread[:])
-
-        ln_flipped = flipped.tile([P, P], BF16, name="bank")
-        nc.tensor.transpose(ln_flipped[:], ln_rows[:], ident_bf16[:])
-        ln_cols = const.tile([P, 2 * PACK], F32)
-        nc.scalar.copy(out=ln_cols[:], in_=ln_flipped[:, 0 : 2 * PACK])
+            b, first, count = GROUPS[g]
+            return slice(b * BATCH_TILES + first + j, b * BATCH_TILES + first + j + 1)
 
         def flip_words(rows):
             row_words = rows.bitcast(F32)
             banks = []
-            for half in range(2):
-                bank = flipped.tile([P, 2, HALF], F32, name="bank")
+            for half in range(rows.shape[1] // 2):
+                bank = flipped.tile([P, 2, 2 * P], F32, name="bank")
                 for jj in range(2):
                     for u in range(2):
                         nc.tensor.transpose(
@@ -126,21 +145,23 @@ def tile_block_pb_t_kernel(tc, attn_out, x, W_proj, b_proj, g2, beta2, W1, b1, o
 
         def copy_words(banks, grouped):
             grouped_words = grouped.bitcast(F32)
-            for half in range(2):
+            for half, bank in enumerate(banks):
                 nc.scalar.copy(
-                    out=grouped_words[:, half * HALF : (half + 1) * HALF, :],
-                    in_=banks[half][:].rearrange("p u w -> p w u"),
+                    out=grouped_words[:, half * 2 * P : (half + 1) * 2 * P, :],
+                    in_=bank[:].rearrange("p u w -> p w u"),
                 )
 
-        def quantise(grouped, operand):
+        def quantise(grouped, operand, cols):
             codes, scales = operand
             nc.vector.quantize_mx(
-                out=codes[:].bitcast(FP8X4), scales=scales[:], in_=grouped.rearrange("p w t -> p (w t)")
+                out=codes[:, 0:cols].bitcast(FP8X4),
+                scales=scales[:, 0:cols],
+                in_=grouped[:, 0:cols, :].rearrange("p w t -> p (w t)"),
             )
 
         def mx_operand(pool, name):
-            codes = pool.tile([P, GROUP_TOKENS], U32, name=name + "_codes", align_bytes=64)
-            scales = pool.tile([P, GROUP_TOKENS], U8, name=name + "_scales", align_bytes=64)
+            codes = pool.tile([P, WIDEST], U32, name=name + "_codes", align_bytes=64)
+            scales = pool.tile([P, WIDEST], U8, name=name + "_scales", align_bytes=64)
             return codes, scales
 
         def matmul_mx_tile(acc, tokens_operand, j, weight_operand):
@@ -155,11 +176,26 @@ def tile_block_pb_t_kernel(tc, attn_out, x, W_proj, b_proj, g2, beta2, W1, b1, o
                 stop=True,
             )
 
-        wp_grouped = pairs.tile([P, D, PACK], BF16, name="a_grouped", align_bytes=64)
-        copy_words(flip_words(wp_rows[:]), wp_grouped[:])
-        wp_operand = mx_operand(const, "wp")
-        quantise(wp_grouped[:], wp_operand)
+        b_proj_held = held.tile([P, 1, D], F32)
+        b_proj_bcast = const.tile([P, D], F32)
+        b1_bcast = const.tile([P, D], F32)
+        ln_cols = const.tile([P, 2 * PACK], F32)
 
+        def spread_b_proj():
+            nc.tensor.matmul(out=b_proj_held[:, 0, :], lhsT=ones[:], rhs=bias_rows[:, 0, :], start=True, stop=True)
+
+        def copy_b_proj():
+            nc.scalar.copy(out=b_proj_bcast[:], in_=b_proj_held[:, 0, :])
+
+        def spread_b1_and_ln():
+            spread = sums.tile([P, D], F32, name="acc")
+            nc.tensor.matmul(out=spread[:], lhsT=ones[:], rhs=bias_rows[:, 1, :], start=True, stop=True)
+            nc.scalar.copy(out=b1_bcast[:], in_=spread[:])
+            ln_flipped = flipped.tile([P, P], BF16, name="bank")
+            nc.tensor.transpose(ln_flipped[:], ln_rows[:], ident_bf16[:])
+            nc.scalar.copy(out=ln_cols[:], in_=ln_flipped[:, 0 : 2 * PACK])
+
+        wp_operand = mx_operand(const, "wp")
         w1_operand = mx_operand(const, "w1")
         w1_grouped = const.tile([P, D, PACK], BF16, align_bytes=64)
         w1_ordered = const.tile([P, PACK, D], BF16)
@@ -173,7 +209,7 @@ def tile_block_pb_t_kernel(tc, attn_out, x, W_proj, b_proj, g2, beta2, W1, b1, o
 
         def flip_w1():
             for half in range(2):
-                bank = flipped.tile([P, PACK, HALF], BF16, name="bank")
+                bank = flipped.tile([P, PACK, 2 * P], BF16, name="bank")
                 for cc in range(2):
                     for t in range(PACK):
                         nc.tensor.transpose(
@@ -182,45 +218,59 @@ def tile_block_pb_t_kernel(tc, attn_out, x, W_proj, b_proj, g2, beta2, W1, b1, o
                             ident_bf16[:],
                         )
                 nc.scalar.copy(
-                    out=w1_grouped[:, half * HALF : (half + 1) * HALF, :],
+                    out=w1_grouped[:, half * 2 * P : (half + 1) * 2 * P, :],
                     in_=bank[:].rearrange("p t n -> p n t"),
                 )
 
         a_banks, a_grouped, a_operand, x_mid = {}, {}, {}, {}
         normed, h_banks, h_planes, h_grouped, h_operand, hidden = {}, {}, {}, {}, {}, {}
 
-        def add_bias(g):
-            if not 0 <= g < GROUPS:
-                return
-            x_mid[g] = resident.tile([P, GROUP_TILES, D], F32, name="x_mid_%d" % g)
-            nc.vector.tensor_tensor(
-                out=x_mid[g][:],
-                in0=x_rows[g][:],
-                in1=b_proj_bcast[:].to_broadcast([P, GROUP_TILES, D]),
-                op=ALU.add,
-            )
+        def exists(g):
+            return 0 <= g < len(GROUPS)
 
         def flip_attention(g):
-            if not 0 <= g < GROUPS:
+            if not exists(g):
                 return
-            a_banks[g] = flip_words(attn_rows[g][:])
+            b, tiles = batch_tiles(g)
+            a_banks[g] = flip_words(attn_rows[b][:, tiles, :])
 
         def copy_attention(g):
-            if not 0 <= g < GROUPS:
+            if not exists(g):
                 return
-            a_grouped[g] = pairs.tile([P, GROUP_TOKENS, PACK], BF16, name="a_grouped", align_bytes=64)
+            a_grouped[g] = pairs.tile([P, WIDEST, PACK], BF16, name="a_grouped", align_bytes=64)
             copy_words(a_banks[g], a_grouped[g][:])
 
         def quantise_attention(g):
-            if not 0 <= g < GROUPS:
+            if not exists(g):
                 return
-            a_operand[g] = mx_operand(triples, "a")
-            quantise(a_grouped[g][:], a_operand[g])
+            a_operand[g] = mx_operand(pairs, "a")
+            quantise(a_grouped[g], a_operand[g], width(g))
+
+        def release_gpsimd():
+            nc.vector.tensor_copy(out=b_proj_bcast[:, 0:1], in_=b_proj_held[:, 0, 0:1])
+
+        def add_bias(g, for_gpsimd):
+            if not exists(g):
+                return
+            b, tiles = batch_tiles(g)
+            x_mid[g] = sixes.tile([P, BATCH_TILES, D], F32, name="x_mid")
+            mine = GROUPS[g][2] - for_gpsimd
+            if mine > 0:
+                nc.vector.tensor_tensor(
+                    out=x_mid[g][:, 0:mine, :],
+                    in0=x_rows[b][:, tiles.start : tiles.start + mine, :],
+                    in1=b_proj_held[:].to_broadcast([P, mine, D]),
+                    op=ALU.add,
+                )
+            for j in range(mine, GROUPS[g][2]):
+                nc.gpsimd.tensor_tensor(
+                    out=x_mid[g][:, j, :], in0=x_rows[b][:, tiles.start + j, :], in1=b_proj_bcast[:], op=ALU.add
+                )
 
         def project_attention(g):
-            if not 0 <= g < GROUPS:
+            if not exists(g):
                 return
-            for j in range(GROUP_TILES):
+            for j in tiles_of(g):
                 acc = sums.tile([P, D], F32, name="acc")
                 matmul_mx_tile(acc, a_operand[g], j, wp_operand)
                 nc.vector.scalar_tensor_tensor(
@@ -234,11 +284,11 @@ def tile_block_pb_t_kernel(tc, attn_out, x, W_proj, b_proj, g2, beta2, W1, b1, o
                 )
 
         def variance(g):
-            if not 0 <= g < GROUPS:
+            if not exists(g):
                 return
             nc.scalar.mul(out=neg_mean[:, stat_cols(g)], in_=row_sum[:, stat_cols(g)], mul=-1.0 / D)
-            squares = pairs.tile([P, GROUP_TILES, D], BF16, name="squares")
-            for j in range(GROUP_TILES):
+            squares = pairs.tile([P, BATCH_TILES, D], BF16, name="squares")
+            for j in tiles_of(g):
                 nc.scalar.activation(
                     out=squares[:, j, :],
                     in_=x_mid[g][:, j, :],
@@ -247,12 +297,13 @@ def tile_block_pb_t_kernel(tc, attn_out, x, W_proj, b_proj, g2, beta2, W1, b1, o
                     scale=1.0,
                     accum_out=sq_sum[:, stat_col(g, j)],
                 )
-            nc.sync.dma_start(out=x_mid_groups[g], in_=x_mid[g][:])
+            b, tiles = batch_tiles(g)
+            nc.sync.dma_start(out=x_mid_batches[b][:, tiles, :], in_=x_mid[g][:, 0 : GROUPS[g][2], :])
 
-        def reciprocal_std(g):
-            if not 0 <= g < GROUPS:
+        def add_eps(g):
+            if not exists(g):
                 return
-            nc.gpsimd.tensor_scalar(
+            nc.vector.tensor_scalar(
                 out=var_eps[:, stat_cols(g)],
                 in0=sq_sum[:, stat_cols(g)],
                 scalar1=1.0 / D,
@@ -260,16 +311,23 @@ def tile_block_pb_t_kernel(tc, attn_out, x, W_proj, b_proj, g2, beta2, W1, b1, o
                 op0=ALU.mult,
                 op1=ALU.add,
             )
+
+        def reciprocal_std(g):
+            if not exists(g):
+                return
             nc.gpsimd.tensor_tensor(
-                out=rstd[:, stat_cols(g)], in0=var_eps[:, stat_cols(g)], in1=neg_half[:], op=ALU.pow
+                out=rstd[:, stat_cols(g)],
+                in0=var_eps[:, stat_cols(g)],
+                in1=neg_half[:, 0 : GROUPS[g][2]],
+                op=ALU.pow,
             )
 
         def normalise(g):
-            if not 0 <= g < GROUPS:
+            if not exists(g):
                 return
-            normed[g] = pairs.tile([P, GROUP_TILES, D], F32, name="normed")
-            for j in range(GROUP_TILES):
-                nc.gpsimd.tensor_scalar(
+            normed[g] = pairs.tile([P, BATCH_TILES, D], F32, name="normed")
+            for j in tiles_of(g):
+                nc.vector.tensor_scalar(
                     out=normed[g][:, j, :].rearrange("p (t q r) -> p t q r", t=PACK, r=RUN),
                     in0=x_mid[g][:, j, :].rearrange("p (q t r) -> p t q r", t=PACK, r=RUN),
                     scalar1=neg_mean[:, stat_col(g, j)],
@@ -279,83 +337,105 @@ def tile_block_pb_t_kernel(tc, attn_out, x, W_proj, b_proj, g2, beta2, W1, b1, o
                 )
 
         def flip_normed(g):
-            if not 0 <= g < GROUPS:
+            if not exists(g):
                 return
             h_banks[g] = []
             for t in range(PACK):
-                bank = flipped.tile([P, GROUP_TOKENS], F32, name="bank")
-                for j in range(GROUP_TILES):
+                bank = flipped.tile([P, WIDEST], F32, name="bank")
+                for j in tiles_of(g):
                     nc.tensor.transpose(
                         bank[:, j * P : (j + 1) * P], normed[g][:, j, t * P : (t + 1) * P], ident_f32[:]
                     )
                 h_banks[g].append(bank)
 
         def scale_shift(g):
-            if not 0 <= g < GROUPS:
+            if not exists(g):
                 return
-            h_planes[g] = pairs.tile([P, PACK, GROUP_TOKENS], BF16, name="h_planes")
+            h_planes[g] = pairs.tile([P, PACK, WIDEST], BF16, name="h_planes")
             for t in range(PACK):
                 nc.scalar.activation(
-                    out=h_planes[g][:, t, :],
-                    in_=h_banks[g][t][:],
+                    out=h_planes[g][:, t, 0 : width(g)],
+                    in_=h_banks[g][t][:, 0 : width(g)],
                     func=ACT.Identity,
                     scale=ln_cols[:, t : t + 1],
                     bias=ln_cols[:, PACK + t : PACK + t + 1],
                 )
 
         def regroup_h(g):
-            if not 0 <= g < GROUPS:
+            if not exists(g):
                 return
-            h_grouped[g] = pairs.tile([P, GROUP_TOKENS, PACK], BF16, name="h_grouped", align_bytes=64)
+            h_grouped[g] = pairs.tile([P, WIDEST, PACK], BF16, name="h_grouped", align_bytes=64)
             nc.vector.tensor_copy(
-                out=h_grouped[g][:].rearrange("p (c i) t -> p c t i", i=4),
-                in_=h_planes[g][:].rearrange("p t (c i) -> p c t i", i=4),
+                out=h_grouped[g][:, 0 : width(g), :].rearrange("p (c i) t -> p c t i", i=4),
+                in_=h_planes[g][:, :, 0 : width(g)].rearrange("p t (c i) -> p c t i", i=4),
             )
 
         def quantise_h(g):
-            if not 0 <= g < GROUPS:
+            if not exists(g):
                 return
-            h_operand[g] = mx_operand(triples, "h")
-            quantise(h_grouped[g][:], h_operand[g])
+            h_operand[g] = mx_operand(pairs, "h")
+            quantise(h_grouped[g], h_operand[g], width(g))
 
         def project_h(g):
-            if not 0 <= g < GROUPS:
+            if not exists(g):
                 return
-            hidden[g] = triples.tile([P, GROUP_TILES, D], F32, name="hidden")
-            for j in range(GROUP_TILES):
+            hidden[g] = triples.tile([P, BATCH_TILES, D], F32, name="hidden")
+            for j in tiles_of(g):
                 acc = sums.tile([P, D], F32, name="acc")
                 matmul_mx_tile(acc, h_operand[g], j, w1_operand)
-                nc.vector.tensor_tensor(
-                    out=hidden[g][:, j, :], in0=acc[:], in1=b1_bcast[:], op=ALU.add
-                )
+                nc.vector.tensor_tensor(out=hidden[g][:, j, :], in0=acc[:], in1=b1_bcast[:], op=ALU.add)
 
         def gelu(g):
-            if not 0 <= g < GROUPS:
+            if not exists(g):
                 return
-            for j in range(GROUP_TILES):
+            b, tiles = batch_tiles(g)
+            for j in tiles_of(g):
                 nc.scalar.activation(out=hidden[g][:, j, :], in_=hidden[g][:, j, :], func=ACT.Gelu)
-                nc.sync.dma_start(out=u_groups[g][:, j, :], in_=hidden[g][:, j, :])
+                nc.sync.dma_start(out=u_batches[b][:, tiles.start + j, :], in_=hidden[g][:, j, :])
 
-        W1_STEP = 2
-        for step in range(-3, GROUPS + 5):
-            project_attention(step)
-            normalise(step - 1)
-            project_h(step - 5)
-            scale_shift(step - 2)
-            copy_attention(step + 2)
-            if step == W1_STEP - 1:
-                order_w1()
-            if step == W1_STEP:
-                flip_w1()
-            variance(step)
-            quantise_h(step - 3)
-            quantise_attention(step + 2)
-            if step == W1_STEP + 1:
-                quantise(w1_grouped[:], w1_operand)
-            flip_normed(step - 1)
-            gelu(step - 5)
-            add_bias(step + 3)
-            flip_attention(step + 3)
-            reciprocal_std(step)
-            regroup_h(step - 2)
-            load(step + 6)
+        def psum_tiles(step):
+            return sum(GROUPS[g][2] for g in (step, step - 3) if exists(g))
+
+        def for_gpsimd(step):
+            if not exists(step + 2):
+                return 0
+            return min(max(psum_tiles(step) // 2 - 1, 0), GROUPS[step + 2][2])
+
+        with tc.manual_schedule():
+            spread_b_proj()
+            wp_grouped = pairs.tile([P, WIDEST, PACK], BF16, name="a_grouped", align_bytes=64)
+            wp_banks = flip_words(wp_rows[:])
+            copy_words(wp_banks, wp_grouped[:])
+            flip_attention(0)
+            copy_attention(0)
+            add_bias(0, 0)
+            add_bias(1, 0)
+            quantise(wp_grouped, wp_operand, D)
+            quantise_attention(0)
+            copy_b_proj()
+            for step in range(len(GROUPS) + 3):
+                scale_shift(step - 2)
+                project_attention(step)
+                flip_attention(step + 1)
+                copy_attention(step + 1)
+                if step == 0:
+                    spread_b1_and_ln()
+                if step == 2:
+                    flip_w1()
+                add_bias(step + 2, for_gpsimd(step))
+                variance(step)
+                project_h(step - 3)
+                gelu(step - 3)
+                normalise(step - 1)
+                flip_normed(step - 1)
+                quantise_attention(step + 1)
+                if step == 1:
+                    order_w1()
+                if step == 2:
+                    quantise(w1_grouped, w1_operand, D)
+                regroup_h(step - 2)
+                add_eps(step)
+                reciprocal_std(step)
+                if for_gpsimd(step + 1) > 0:
+                    release_gpsimd()
+                quantise_h(step - 2)

@@ -48,8 +48,7 @@ def tile_block_pb_t_kernel(tc, attn_out, x, W_proj, b_proj, g2, beta2, W1, b1, o
         triples = ctx.enter_context(tc.tile_pool(name="triples", bufs=3))
         sixes = ctx.enter_context(tc.tile_pool(name="sixes", bufs=6))
         flipped = ctx.enter_context(tc.psum_pool(name="flipped", bufs=4))
-        sums = ctx.enter_context(tc.psum_pool(name="sums", bufs=3))
-        held = ctx.enter_context(tc.psum_pool(name="held", bufs=1))
+        sums = ctx.enter_context(tc.psum_pool(name="sums", bufs=4))
 
         attn_rows, x_rows = {}, {}
 
@@ -176,16 +175,14 @@ def tile_block_pb_t_kernel(tc, attn_out, x, W_proj, b_proj, g2, beta2, W1, b1, o
                 stop=True,
             )
 
-        b_proj_held = held.tile([P, 1, D], F32)
-        b_proj_bcast = const.tile([P, D], F32)
+        b_proj_bcast = const.tile([P, 1, D], F32)
         b1_bcast = const.tile([P, D], F32)
         ln_cols = const.tile([P, 2 * PACK], F32)
 
         def spread_b_proj():
-            nc.tensor.matmul(out=b_proj_held[:, 0, :], lhsT=ones[:], rhs=bias_rows[:, 0, :], start=True, stop=True)
-
-        def copy_b_proj():
-            nc.scalar.copy(out=b_proj_bcast[:], in_=b_proj_held[:, 0, :])
+            spread = sums.tile([P, D], F32, name="acc")
+            nc.tensor.matmul(out=spread[:], lhsT=ones[:], rhs=bias_rows[:, 0, :], start=True, stop=True)
+            nc.scalar.copy(out=b_proj_bcast[:, 0, :], in_=spread[:])
 
         def spread_b1_and_ln():
             spread = sums.tile([P, D], F32, name="acc")
@@ -222,8 +219,13 @@ def tile_block_pb_t_kernel(tc, attn_out, x, W_proj, b_proj, g2, beta2, W1, b1, o
                     in_=bank[:].rearrange("p t n -> p n t"),
                 )
 
-        a_banks, a_grouped, a_operand, x_mid = {}, {}, {}, {}
+        a_banks, a_grouped, a_operand, a_sums = {}, {}, {}, {}
+        x_mid = {}
         normed, h_banks, h_planes, h_grouped, h_operand, hidden = {}, {}, {}, {}, {}, {}
+
+        def make_x_mid(g):
+            if exists(g):
+                x_mid[g] = sixes.tile([P, BATCH_TILES, D], F32, name="x_mid")
 
         def exists(g):
             return 0 <= g < len(GROUPS)
@@ -237,45 +239,54 @@ def tile_block_pb_t_kernel(tc, attn_out, x, W_proj, b_proj, g2, beta2, W1, b1, o
         def copy_attention(g):
             if not exists(g):
                 return
-            a_grouped[g] = pairs.tile([P, WIDEST, PACK], BF16, name="a_grouped", align_bytes=64)
+            a_grouped[g] = triples.tile([P, WIDEST, PACK], BF16, name="a_grouped", align_bytes=64)
             copy_words(a_banks[g], a_grouped[g][:])
 
         def quantise_attention(g):
             if not exists(g):
                 return
-            a_operand[g] = mx_operand(pairs, "a")
+            a_operand[g] = mx_operand(triples, "a")
             quantise(a_grouped[g], a_operand[g], width(g))
 
         def release_gpsimd():
-            nc.vector.tensor_copy(out=b_proj_bcast[:, 0:1], in_=b_proj_held[:, 0, 0:1])
+            nc.vector.tensor_copy(out=b_proj_bcast[:, 0, 0:1], in_=b_proj_bcast[:, 0, 0:1])
 
-        def add_bias(g, for_gpsimd):
+        def add_bias(g, tiles):
+            if not exists(g) or len(tiles) == 0:
+                return
+            b, first, count = GROUPS[g]
+            nc.vector.tensor_tensor(
+                out=x_mid[g][:, tiles.start : tiles.stop, :],
+                in0=x_rows[b][:, first + tiles.start : first + tiles.stop, :],
+                in1=b_proj_bcast[:].to_broadcast([P, len(tiles), D]),
+                op=ALU.add,
+            )
+
+        def add_bias_on_gpsimd(g, tiles):
             if not exists(g):
                 return
-            b, tiles = batch_tiles(g)
-            x_mid[g] = sixes.tile([P, BATCH_TILES, D], F32, name="x_mid")
-            mine = GROUPS[g][2] - for_gpsimd
-            if mine > 0:
-                nc.vector.tensor_tensor(
-                    out=x_mid[g][:, 0:mine, :],
-                    in0=x_rows[b][:, tiles.start : tiles.start + mine, :],
-                    in1=b_proj_held[:].to_broadcast([P, mine, D]),
-                    op=ALU.add,
-                )
-            for j in range(mine, GROUPS[g][2]):
+            b, first, count = GROUPS[g]
+            for j in tiles:
                 nc.gpsimd.tensor_tensor(
-                    out=x_mid[g][:, j, :], in0=x_rows[b][:, tiles.start + j, :], in1=b_proj_bcast[:], op=ALU.add
+                    out=x_mid[g][:, j, :], in0=x_rows[b][:, first + j, :], in1=b_proj_bcast[:, 0, :], op=ALU.add
                 )
 
         def project_attention(g):
             if not exists(g):
                 return
+            a_sums[g] = []
             for j in tiles_of(g):
                 acc = sums.tile([P, D], F32, name="acc")
                 matmul_mx_tile(acc, a_operand[g], j, wp_operand)
+                a_sums[g].append(acc)
+
+        def add_attention(g):
+            if not exists(g):
+                return
+            for j in tiles_of(g):
                 nc.vector.scalar_tensor_tensor(
                     out=x_mid[g][:, j, :],
-                    in0=acc[:],
+                    in0=a_sums[g][j][:],
                     scalar=1.0,
                     in1=x_mid[g][:, j, :],
                     op0=ALU.mult,
@@ -393,49 +404,68 @@ def tile_block_pb_t_kernel(tc, attn_out, x, W_proj, b_proj, g2, beta2, W1, b1, o
                 nc.scalar.activation(out=hidden[g][:, j, :], in_=hidden[g][:, j, :], func=ACT.Gelu)
                 nc.sync.dma_start(out=u_batches[b][:, tiles.start + j, :], in_=hidden[g][:, j, :])
 
-        def psum_tiles(step):
-            return sum(GROUPS[g][2] for g in (step, step - 3) if exists(g))
+        last = len(GROUPS) - 1
 
-        def for_gpsimd(step):
-            if not exists(step + 2):
-                return 0
-            return min(max(psum_tiles(step) // 2 - 1, 0), GROUPS[step + 2][2])
+        def share(g):
+            return 0 if g < 4 or not exists(g) else GROUPS[g][2] // 2
 
         with tc.manual_schedule():
+            for g in range(4):
+                make_x_mid(g)
             spread_b_proj()
-            wp_grouped = pairs.tile([P, WIDEST, PACK], BF16, name="a_grouped", align_bytes=64)
+            wp_grouped = triples.tile([P, WIDEST, PACK], BF16, name="a_grouped", align_bytes=64)
             wp_banks = flip_words(wp_rows[:])
             copy_words(wp_banks, wp_grouped[:])
             flip_attention(0)
             copy_attention(0)
-            add_bias(0, 0)
-            add_bias(1, 0)
+            flip_attention(1)
+            copy_attention(1)
+            add_bias(0, tiles_of(0))
+            add_bias(1, tiles_of(1))
             quantise(wp_grouped, wp_operand, D)
             quantise_attention(0)
-            copy_b_proj()
+            project_attention(0)
+            add_bias(2, tiles_of(2))
+            quantise_attention(1)
+            spread_b1_and_ln()
             for step in range(len(GROUPS) + 3):
-                scale_shift(step - 2)
-                project_attention(step)
-                flip_attention(step + 1)
-                copy_attention(step + 1)
-                if step == 0:
-                    spread_b1_and_ln()
+                if step <= last:
+                    scale_shift(step - 2)
+                add_attention(step)
+                make_x_mid(step + 4)
+                flip_attention(step + 2)
+                copy_attention(step + 2)
+                variance(step)
+                if step < last:
+                    project_h(step - 3)
+                add_bias_on_gpsimd(step + 2, range(share(step + 2)))
                 if step == 2:
                     flip_w1()
-                add_bias(step + 2, for_gpsimd(step))
-                variance(step)
-                project_h(step - 3)
-                gelu(step - 3)
+                if step < last:
+                    gelu(step - 3)
                 normalise(step - 1)
+                project_attention(step + 1)
                 flip_normed(step - 1)
-                quantise_attention(step + 1)
+                if step >= last:
+                    scale_shift(step - 1)
+                if step == 0:
+                    add_bias(3, tiles_of(3))
                 if step == 1:
                     order_w1()
+                regroup_h(step - 2)
+                quantise_attention(step + 2)
+                if 2 <= step and exists(step + 2):
+                    add_bias(step + 2, range(share(step + 2), GROUPS[step + 2][2]))
+                if step < last:
+                    add_eps(step)
+                    reciprocal_std(step)
+                    if share(step + 3) > 0:
+                        release_gpsimd()
                 if step == 2:
                     quantise(w1_grouped, w1_operand, D)
-                regroup_h(step - 2)
-                add_eps(step)
-                reciprocal_std(step)
-                if for_gpsimd(step + 1) > 0:
-                    release_gpsimd()
                 quantise_h(step - 2)
+                if step >= last:
+                    add_eps(step)
+                    reciprocal_std(step)
+                    project_h(step - 3)
+                    gelu(step - 3)

@@ -67,13 +67,16 @@ def tile_block_pb_t_kernel(tc, attn_out, x, W_proj, b_proj, g2, beta2, W1, b1, o
         whole = slice(0, BATCH_TILES)
         bias_rows = const.tile([P, 2, D], BF16)
         nc.vector.memset(bias_rows[:, 0, :], 0.0)
-        load_x(0, whole)
+        load_x(0, early)
         nc.sync.dma_start(out=bias_rows[0:1, 0, :], in_=b_proj.rearrange("(o d) -> o d", o=1))
         wp_rows = const.tile([P, PACK, D], BF16)
         nc.sync.dma_start(out=wp_rows[:], in_=W_proj.rearrange("(c p) k -> p c k", p=P))
+        load_x(0, late)
         load_attn(0, early)
         load_attn(0, late)
         load_x(1, whole)
+        load_attn(1, whole)
+        load_x(2, whole)
         nc.vector.memset(bias_rows[:, 1, :], 0.0)
         ln_rows = const.tile([P, P], BF16)
         nc.vector.memset(ln_rows[:], 0.0)
@@ -83,10 +86,10 @@ def tile_block_pb_t_kernel(tc, attn_out, x, W_proj, b_proj, g2, beta2, W1, b1, o
                 out=ln_rows[i * PACK : (i + 1) * PACK, :].rearrange("t (q r) -> t q r", r=RUN),
                 in_=vec.rearrange("(q t r) -> t q r", t=PACK, r=RUN),
             )
-        load_attn(1, whole)
         w1_rows = const.tile([P, PACK, D], BF16)
         nc.sync.dma_start(out=w1_rows[:], in_=W1.rearrange("(c p) k -> p c k", p=P))
-        for b in range(2, BATCHES):
+        load_attn(2, whole)
+        for b in range(3, BATCHES):
             load_x(b, whole)
             load_attn(b, whole)
 
@@ -180,9 +183,10 @@ def tile_block_pb_t_kernel(tc, attn_out, x, W_proj, b_proj, g2, beta2, W1, b1, o
         ln_cols = const.tile([P, 2 * PACK], F32)
 
         def spread_b_proj():
-            spread = sums.tile([P, D], F32, name="acc")
-            nc.tensor.matmul(out=spread[:], lhsT=ones[:], rhs=bias_rows[:, 0, :], start=True, stop=True)
-            nc.scalar.copy(out=b_proj_bcast[:, 0, :], in_=spread[:])
+            spread = sums.tile([P, 1, D], F32, name="acc")
+            nc.tensor.matmul(out=spread[:, 0, :], lhsT=ones[:], rhs=bias_rows[:, 0, :], start=True, stop=True)
+            nc.scalar.copy(out=b_proj_bcast[:], in_=spread[:])
+            return spread
 
         def spread_b1_and_ln():
             spread = sums.tile([P, D], F32, name="acc")
@@ -199,7 +203,7 @@ def tile_block_pb_t_kernel(tc, attn_out, x, W_proj, b_proj, g2, beta2, W1, b1, o
 
         def order_w1():
             for c in range(PACK):
-                nc.vector.tensor_copy(
+                nc.scalar.copy(
                     out=w1_ordered[:, c, :].rearrange("p (t q r) -> p t q r", t=PACK, r=RUN),
                     in_=w1_rows[:, c, :].rearrange("p (q t r) -> p t q r", t=PACK, r=RUN),
                 )
@@ -251,25 +255,27 @@ def tile_block_pb_t_kernel(tc, attn_out, x, W_proj, b_proj, g2, beta2, W1, b1, o
         def release_gpsimd():
             nc.vector.tensor_copy(out=b_proj_bcast[:, 0, 0:1], in_=b_proj_bcast[:, 0, 0:1])
 
-        def add_bias(g, tiles):
+        def add_bias(g, tiles, bias=b_proj_bcast):
             if not exists(g) or len(tiles) == 0:
                 return
             b, first, count = GROUPS[g]
             nc.vector.tensor_tensor(
                 out=x_mid[g][:, tiles.start : tiles.stop, :],
                 in0=x_rows[b][:, first + tiles.start : first + tiles.stop, :],
-                in1=b_proj_bcast[:].to_broadcast([P, len(tiles), D]),
+                in1=bias[:].to_broadcast([P, len(tiles), D]),
                 op=ALU.add,
             )
 
         def add_bias_on_gpsimd(g, tiles):
-            if not exists(g):
+            if not exists(g) or len(tiles) == 0:
                 return
             b, first, count = GROUPS[g]
-            for j in tiles:
-                nc.gpsimd.tensor_tensor(
-                    out=x_mid[g][:, j, :], in0=x_rows[b][:, first + j, :], in1=b_proj_bcast[:, 0, :], op=ALU.add
-                )
+            nc.gpsimd.tensor_tensor(
+                out=x_mid[g][:, tiles.start : tiles.stop, :],
+                in0=x_rows[b][:, first + tiles.start : first + tiles.stop, :],
+                in1=b_proj_bcast[:].to_broadcast([P, len(tiles), D]),
+                op=ALU.add,
+            )
 
         def project_attention(g):
             if not exists(g):
@@ -297,17 +303,17 @@ def tile_block_pb_t_kernel(tc, attn_out, x, W_proj, b_proj, g2, beta2, W1, b1, o
         def variance(g):
             if not exists(g):
                 return
-            nc.scalar.mul(out=neg_mean[:, stat_cols(g)], in_=row_sum[:, stat_cols(g)], mul=-1.0 / D)
             squares = pairs.tile([P, BATCH_TILES, D], BF16, name="squares")
             for j in tiles_of(g):
                 nc.scalar.activation(
                     out=squares[:, j, :],
                     in_=x_mid[g][:, j, :],
                     func=ACT.Square,
-                    bias=neg_mean[:, stat_col(g, j)],
-                    scale=1.0,
+                    bias=row_sum[:, stat_col(g, j)],
+                    scale=-float(D),
                     accum_out=sq_sum[:, stat_col(g, j)],
                 )
+            nc.scalar.mul(out=neg_mean[:, stat_cols(g)], in_=row_sum[:, stat_cols(g)], mul=-1.0 / D)
             b, tiles = batch_tiles(g)
             nc.sync.dma_start(out=x_mid_batches[b][:, tiles, :], in_=x_mid[g][:, 0 : GROUPS[g][2], :])
 
@@ -317,7 +323,7 @@ def tile_block_pb_t_kernel(tc, attn_out, x, W_proj, b_proj, g2, beta2, W1, b1, o
             nc.vector.tensor_scalar(
                 out=var_eps[:, stat_cols(g)],
                 in0=sq_sum[:, stat_cols(g)],
-                scalar1=1.0 / D,
+                scalar1=1.0 / D**3,
                 scalar2=LN_EPS,
                 op0=ALU.mult,
                 op1=ALU.add,
@@ -372,14 +378,25 @@ def tile_block_pb_t_kernel(tc, attn_out, x, W_proj, b_proj, g2, beta2, W1, b1, o
                     bias=ln_cols[:, PACK + t : PACK + t + 1],
                 )
 
-        def regroup_h(g):
+        def regroup(copy, g, tokens):
+            copy(
+                out=h_grouped[g][:, tokens, :].rearrange("p (c i) t -> p c t i", i=4),
+                in_=h_planes[g][:, :, tokens].rearrange("p t (c i) -> p c t i", i=4),
+            )
+
+        def scalars_tokens(g):
+            return slice(width(g) - P * (GROUPS[g][2] // BATCH_TILES), width(g))
+
+        def regroup_on_scalar(g):
             if not exists(g):
                 return
             h_grouped[g] = pairs.tile([P, WIDEST, PACK], BF16, name="h_grouped", align_bytes=64)
-            nc.vector.tensor_copy(
-                out=h_grouped[g][:, 0 : width(g), :].rearrange("p (c i) t -> p c t i", i=4),
-                in_=h_planes[g][:, :, 0 : width(g)].rearrange("p t (c i) -> p c t i", i=4),
-            )
+            if GROUPS[g][2] == BATCH_TILES:
+                regroup(nc.scalar.copy, g, scalars_tokens(g))
+
+        def regroup_h(g):
+            if exists(g):
+                regroup(nc.vector.tensor_copy, g, slice(0, scalars_tokens(g).start))
 
         def quantise_h(g):
             if not exists(g):
@@ -407,12 +424,12 @@ def tile_block_pb_t_kernel(tc, attn_out, x, W_proj, b_proj, g2, beta2, W1, b1, o
         last = len(GROUPS) - 1
 
         def share(g):
-            return 0 if g < 4 or not exists(g) else GROUPS[g][2] // 2
+            return 0 if g < 4 or not exists(g) else (2 * GROUPS[g][2]) // 4
 
         with tc.manual_schedule():
             for g in range(4):
                 make_x_mid(g)
-            spread_b_proj()
+            spread = spread_b_proj()
             wp_grouped = triples.tile([P, WIDEST, PACK], BF16, name="a_grouped", align_bytes=64)
             wp_banks = flip_words(wp_rows[:])
             copy_words(wp_banks, wp_grouped[:])
@@ -420,27 +437,31 @@ def tile_block_pb_t_kernel(tc, attn_out, x, W_proj, b_proj, g2, beta2, W1, b1, o
             copy_attention(0)
             flip_attention(1)
             copy_attention(1)
-            add_bias(0, tiles_of(0))
-            add_bias(1, tiles_of(1))
+            add_bias(0, tiles_of(0), spread)
+            add_bias(1, tiles_of(1), spread)
             quantise(wp_grouped, wp_operand, D)
             quantise_attention(0)
             project_attention(0)
             add_bias(2, tiles_of(2))
             quantise_attention(1)
-            spread_b1_and_ln()
             for step in range(len(GROUPS) + 3):
                 if step <= last:
                     scale_shift(step - 2)
+                    regroup_on_scalar(step - 2)
                 add_attention(step)
                 make_x_mid(step + 4)
                 flip_attention(step + 2)
                 copy_attention(step + 2)
                 variance(step)
+                if step == 0:
+                    order_w1()
                 if step < last:
                     project_h(step - 3)
                 add_bias_on_gpsimd(step + 2, range(share(step + 2)))
-                if step == 2:
+                if step == 1:
                     flip_w1()
+                if step == 0:
+                    spread_b1_and_ln()
                 if step < last:
                     gelu(step - 3)
                 normalise(step - 1)
@@ -448,10 +469,9 @@ def tile_block_pb_t_kernel(tc, attn_out, x, W_proj, b_proj, g2, beta2, W1, b1, o
                 flip_normed(step - 1)
                 if step >= last:
                     scale_shift(step - 1)
+                    regroup_on_scalar(step - 1)
                 if step == 0:
                     add_bias(3, tiles_of(3))
-                if step == 1:
-                    order_w1()
                 regroup_h(step - 2)
                 quantise_attention(step + 2)
                 if 2 <= step and exists(step + 2):

@@ -24,9 +24,9 @@ LN_EPS = 1e-6
 
 SMALL = BATCH_TILES // 2
 GROUPS = (
-    [(0, 0, SMALL), (0, SMALL, SMALL)]
+    [(0, 0, 2), (0, 2, 2)]
     + [(b, 0, BATCH_TILES) for b in range(1, BATCHES - 1)]
-    + [(BATCHES - 1, 0, SMALL), (BATCHES - 1, SMALL, SMALL)]
+    + [(BATCHES - 1, 0, 4)]
 )
 
 FLOPS = 2 * 2 * TOKENS * D * D
@@ -66,7 +66,11 @@ def tile_block_pb_t_kernel(tc, attn_out, x, W_proj, b_proj, g2, beta2, W1, b1, o
         late = slice(SMALL, BATCH_TILES)
         whole = slice(0, BATCH_TILES)
         bias_rows = const.tile([P, 2, D], BF16)
-        nc.vector.memset(bias_rows[:, 0, :], 0.0)
+        nc.gpsimd.memset(bias_rows[:, 0, :], 0.0)
+        ones = const.tile([P, P], BF16)
+        nc.vector.memset(ones[:], 1.0)
+        ident_f32 = const.tile([P, P], F32)
+        make_identity(nc, ident_f32[:])
         load_x(0, early)
         nc.sync.dma_start(out=bias_rows[0:1, 0, :], in_=b_proj.rearrange("(o d) -> o d", o=1))
         wp_rows = const.tile([P, PACK, D], BF16)
@@ -97,12 +101,8 @@ def tile_block_pb_t_kernel(tc, attn_out, x, W_proj, b_proj, g2, beta2, W1, b1, o
         nc.vector.memset(warm[:], 0.0)
         nc.scalar.activation(out=warm[:], in_=warm[:], func=ACT.Gelu)
 
-        ident_f32 = const.tile([P, P], F32)
-        make_identity(nc, ident_f32[:])
         ident_bf16 = const.tile([P, P], BF16)
         make_identity(nc, ident_bf16[:])
-        ones = const.tile([P, P], BF16)
-        nc.vector.memset(ones[:], 1.0)
         neg_half = const.tile([P, BATCH_TILES], F32)
         nc.vector.memset(neg_half[:], -0.5)
 
@@ -185,7 +185,6 @@ def tile_block_pb_t_kernel(tc, attn_out, x, W_proj, b_proj, g2, beta2, W1, b1, o
         def spread_b_proj():
             spread = sums.tile([P, 1, D], F32, name="acc")
             nc.tensor.matmul(out=spread[:, 0, :], lhsT=ones[:], rhs=bias_rows[:, 0, :], start=True, stop=True)
-            nc.scalar.copy(out=b_proj_bcast[:], in_=spread[:])
             return spread
 
         def spread_b1_and_ln():
@@ -251,9 +250,6 @@ def tile_block_pb_t_kernel(tc, attn_out, x, W_proj, b_proj, g2, beta2, W1, b1, o
                 return
             a_operand[g] = mx_operand(triples, "a")
             quantise(a_grouped[g], a_operand[g], width(g))
-
-        def release_gpsimd():
-            nc.vector.tensor_copy(out=b_proj_bcast[:, 0, 0:1], in_=b_proj_bcast[:, 0, 0:1])
 
         def add_bias(g, tiles, bias=b_proj_bcast):
             if not exists(g) or len(tiles) == 0:
@@ -424,7 +420,7 @@ def tile_block_pb_t_kernel(tc, attn_out, x, W_proj, b_proj, g2, beta2, W1, b1, o
         last = len(GROUPS) - 1
 
         def share(g):
-            return 0 if g < 4 or not exists(g) else (2 * GROUPS[g][2]) // 4
+            return 0 if g < 4 or not exists(g) else 2 if g < 7 else 3
 
         with tc.manual_schedule():
             for g in range(4):
@@ -442,16 +438,18 @@ def tile_block_pb_t_kernel(tc, attn_out, x, W_proj, b_proj, g2, beta2, W1, b1, o
             quantise(wp_grouped, wp_operand, D)
             quantise_attention(0)
             project_attention(0)
-            add_bias(2, tiles_of(2))
+            add_bias(2, tiles_of(2), spread)
+            nc.scalar.copy(out=b_proj_bcast[:], in_=spread[:])
             quantise_attention(1)
             for step in range(len(GROUPS) + 3):
                 if step <= last:
                     scale_shift(step - 2)
-                    regroup_on_scalar(step - 2)
                 add_attention(step)
                 make_x_mid(step + 4)
                 flip_attention(step + 2)
                 copy_attention(step + 2)
+                if step <= last:
+                    regroup_on_scalar(step - 2)
                 variance(step)
                 if step == 0:
                     order_w1()
@@ -474,15 +472,13 @@ def tile_block_pb_t_kernel(tc, attn_out, x, W_proj, b_proj, g2, beta2, W1, b1, o
                     add_bias(3, tiles_of(3))
                 regroup_h(step - 2)
                 quantise_attention(step + 2)
+                if step == 2:
+                    quantise(w1_grouped, w1_operand, D)
                 if 2 <= step and exists(step + 2):
                     add_bias(step + 2, range(share(step + 2), GROUPS[step + 2][2]))
                 if step < last:
                     add_eps(step)
                     reciprocal_std(step)
-                    if share(step + 3) > 0:
-                        release_gpsimd()
-                if step == 2:
-                    quantise(w1_grouped, w1_operand, D)
                 quantise_h(step - 2)
                 if step >= last:
                     add_eps(step)

@@ -153,12 +153,12 @@ def tile_block_pb_t_kernel(tc, attn_out, x, W_proj, b_proj, g2, beta2, W1, b1, o
                     in_=bank[:].rearrange("p u w -> p w u"),
                 )
 
-        def quantise(grouped, operand, cols):
+        def quantise(grouped, operand, start, stop):
             codes, scales = operand
             nc.vector.quantize_mx(
-                out=codes[:, 0:cols].bitcast(FP8X4),
-                scales=scales[:, 0:cols],
-                in_=grouped[:, 0:cols, :].rearrange("p w t -> p (w t)"),
+                out=codes[:, start:stop].bitcast(FP8X4),
+                scales=scales[:, start:stop],
+                in_=grouped[:, start:stop, :].rearrange("p w t -> p (w t)"),
             )
 
         def mx_operand(pool, name):
@@ -190,7 +190,7 @@ def tile_block_pb_t_kernel(tc, attn_out, x, W_proj, b_proj, g2, beta2, W1, b1, o
         def spread_b1_and_ln():
             spread = sums.tile([P, D], F32, name="acc")
             nc.tensor.matmul(out=spread[:], lhsT=ones[:], rhs=bias_rows[:, 1, :], start=True, stop=True)
-            nc.scalar.copy(out=b1_bcast[:], in_=spread[:])
+            nc.vector.tensor_copy(out=b1_bcast[:], in_=spread[:])
             ln_flipped = flipped.tile([P, P], BF16, name="bank")
             nc.tensor.transpose(ln_flipped[:], ln_rows[:], ident_bf16[:])
             nc.scalar.copy(out=ln_cols[:], in_=ln_flipped[:, 0 : 2 * PACK])
@@ -222,8 +222,9 @@ def tile_block_pb_t_kernel(tc, attn_out, x, W_proj, b_proj, g2, beta2, W1, b1, o
                     in_=bank[:].rearrange("p t n -> p n t"),
                 )
 
+        last = len(GROUPS) - 1
         a_banks, a_grouped, a_operand, a_sums = {}, {}, {}, {}
-        x_mid = {}
+        x_mid, h_sums = {}, {}
         normed, h_banks, h_planes, h_grouped, h_operand, hidden = {}, {}, {}, {}, {}, {}
 
         def make_x_mid(g):
@@ -249,7 +250,7 @@ def tile_block_pb_t_kernel(tc, attn_out, x, W_proj, b_proj, g2, beta2, W1, b1, o
             if not exists(g):
                 return
             a_operand[g] = mx_operand(triples, "a")
-            quantise(a_grouped[g], a_operand[g], width(g))
+            quantise(a_grouped[g], a_operand[g], 0, width(g))
 
         def add_bias(g, tiles, bias=b_proj_bcast):
             if not exists(g) or len(tiles) == 0:
@@ -392,22 +393,32 @@ def tile_block_pb_t_kernel(tc, attn_out, x, W_proj, b_proj, g2, beta2, W1, b1, o
 
         def regroup_h(g):
             if exists(g):
-                regroup(nc.vector.tensor_copy, g, slice(0, scalars_tokens(g).start))
+                mine = scalars_tokens(g).start
+                cuts = (0, width(g) // 2, mine) if g > last - 3 else (0, mine)
+                for start, stop in zip(cuts, cuts[1:]):
+                    regroup(nc.vector.tensor_copy, g, slice(start, stop))
 
         def quantise_h(g):
             if not exists(g):
                 return
             h_operand[g] = mx_operand(pairs, "h")
-            quantise(h_grouped[g], h_operand[g], width(g))
+            cuts = (0, width(g) // 2, width(g)) if g > last - 3 else (0, width(g))
+            for start, stop in zip(cuts, cuts[1:]):
+                quantise(h_grouped[g], h_operand[g], start, stop)
 
         def project_h(g):
             if not exists(g):
                 return
+            for j in tiles_of(g):
+                h_sums[g, j] = sums.tile([P, D], F32, name="acc")
+                matmul_mx_tile(h_sums[g, j], h_operand[g], j, w1_operand)
+
+        def add_b1(g):
+            if not exists(g):
+                return
             hidden[g] = triples.tile([P, BATCH_TILES, D], F32, name="hidden")
             for j in tiles_of(g):
-                acc = sums.tile([P, D], F32, name="acc")
-                matmul_mx_tile(acc, h_operand[g], j, w1_operand)
-                nc.vector.tensor_tensor(out=hidden[g][:, j, :], in0=acc[:], in1=b1_bcast[:], op=ALU.add)
+                nc.vector.tensor_tensor(out=hidden[g][:, j, :], in0=h_sums[g, j][:], in1=b1_bcast[:], op=ALU.add)
 
         def gelu(g):
             if not exists(g):
@@ -416,8 +427,6 @@ def tile_block_pb_t_kernel(tc, attn_out, x, W_proj, b_proj, g2, beta2, W1, b1, o
             for j in tiles_of(g):
                 nc.scalar.activation(out=hidden[g][:, j, :], in_=hidden[g][:, j, :], func=ACT.Gelu)
                 nc.sync.dma_start(out=u_batches[b][:, tiles.start + j, :], in_=hidden[g][:, j, :])
-
-        last = len(GROUPS) - 1
 
         def share(g):
             return 0 if g < 4 or not exists(g) else 2 if g < 7 else 3
@@ -435,11 +444,11 @@ def tile_block_pb_t_kernel(tc, attn_out, x, W_proj, b_proj, g2, beta2, W1, b1, o
             copy_attention(1)
             add_bias(0, tiles_of(0), spread)
             add_bias(1, tiles_of(1), spread)
-            quantise(wp_grouped, wp_operand, D)
+            nc.vector.tensor_copy(out=b_proj_bcast[:], in_=spread[:])
+            quantise(wp_grouped, wp_operand, 0, D)
             quantise_attention(0)
             project_attention(0)
             add_bias(2, tiles_of(2), spread)
-            nc.scalar.copy(out=b_proj_bcast[:], in_=spread[:])
             quantise_attention(1)
             for step in range(len(GROUPS) + 3):
                 if step <= last:
@@ -453,8 +462,9 @@ def tile_block_pb_t_kernel(tc, attn_out, x, W_proj, b_proj, g2, beta2, W1, b1, o
                 variance(step)
                 if step == 0:
                     order_w1()
+                project_h(step - 3)
                 if step < last:
-                    project_h(step - 3)
+                    add_b1(step - 3)
                 add_bias_on_gpsimd(step + 2, range(share(step + 2)))
                 if step == 1:
                     flip_w1()
@@ -462,19 +472,21 @@ def tile_block_pb_t_kernel(tc, attn_out, x, W_proj, b_proj, g2, beta2, W1, b1, o
                     spread_b1_and_ln()
                 if step < last:
                     gelu(step - 3)
+                if step == 1:
+                    add_bias(3, tiles_of(3), spread)
+                if step == 2:
+                    add_bias(4, range(share(4), GROUPS[4][2]), spread)
                 normalise(step - 1)
                 project_attention(step + 1)
                 flip_normed(step - 1)
                 if step >= last:
                     scale_shift(step - 1)
                     regroup_on_scalar(step - 1)
-                if step == 0:
-                    add_bias(3, tiles_of(3))
                 regroup_h(step - 2)
                 quantise_attention(step + 2)
                 if step == 2:
-                    quantise(w1_grouped, w1_operand, D)
-                if 2 <= step and exists(step + 2):
+                    quantise(w1_grouped, w1_operand, 0, D)
+                if 3 <= step and exists(step + 2):
                     add_bias(step + 2, range(share(step + 2), GROUPS[step + 2][2]))
                 if step < last:
                     add_eps(step)
@@ -483,5 +495,5 @@ def tile_block_pb_t_kernel(tc, attn_out, x, W_proj, b_proj, g2, beta2, W1, b1, o
                 if step >= last:
                     add_eps(step)
                     reciprocal_std(step)
-                    project_h(step - 3)
+                    add_b1(step - 3)
                     gelu(step - 3)

@@ -71,31 +71,32 @@ def tile_block_pb_t_kernel(tc, attn_out, x, W_proj, b_proj, g2, beta2, W1, b1, o
         nc.vector.memset(ones[:], 1.0)
         ident_f32 = const.tile([P, P], F32)
         make_identity(nc, ident_f32[:])
-        load_x(0, early)
-        nc.sync.dma_start(out=bias_rows[0:1, 0, :], in_=b_proj.rearrange("(o d) -> o d", o=1))
-        wp_rows = const.tile([P, PACK, D], BF16)
-        nc.sync.dma_start(out=wp_rows[:], in_=W_proj.rearrange("(c p) k -> p c k", p=P))
-        load_x(0, late)
-        load_attn(0, early)
-        load_attn(0, late)
-        load_x(1, whole)
-        load_attn(1, whole)
-        load_x(2, whole)
-        nc.vector.memset(bias_rows[:, 1, :], 0.0)
-        ln_rows = const.tile([P, P], BF16)
-        nc.vector.memset(ln_rows[:], 0.0)
-        nc.sync.dma_start(out=bias_rows[0:1, 1, :], in_=b1.rearrange("(o d) -> o d", o=1))
-        for i, vec in enumerate((g2, beta2)):
-            nc.sync.dma_start(
-                out=ln_rows[i * PACK : (i + 1) * PACK, :].rearrange("t (q r) -> t q r", r=RUN),
-                in_=vec.rearrange("(q t r) -> t q r", t=PACK, r=RUN),
-            )
-        w1_rows = const.tile([P, PACK, D], BF16)
-        nc.sync.dma_start(out=w1_rows[:], in_=W1.rearrange("(c p) k -> p c k", p=P))
-        load_attn(2, whole)
-        for b in range(3, BATCHES):
-            load_x(b, whole)
-            load_attn(b, whole)
+        with tc.manual_schedule(engines={mybir.EngineType.SP}):
+            load_x(0, early)
+            nc.sync.dma_start(out=bias_rows[0:1, 0, :], in_=b_proj.rearrange("(o d) -> o d", o=1))
+            wp_rows = const.tile([P, PACK, D], BF16)
+            nc.sync.dma_start(out=wp_rows[:], in_=W_proj.rearrange("(c p) k -> p c k", p=P))
+            load_x(0, late)
+            load_attn(0, early)
+            load_attn(0, late)
+            load_x(1, whole)
+            load_attn(1, whole)
+            load_x(2, whole)
+            nc.vector.memset(bias_rows[:, 1, :], 0.0)
+            ln_rows = const.tile([P, P], BF16)
+            nc.vector.memset(ln_rows[:], 0.0)
+            nc.sync.dma_start(out=bias_rows[0:1, 1, :], in_=b1.rearrange("(o d) -> o d", o=1))
+            for i, vec in enumerate((g2, beta2)):
+                nc.sync.dma_start(
+                    out=ln_rows[i * PACK : (i + 1) * PACK, :].rearrange("t (q r) -> t q r", r=RUN),
+                    in_=vec.rearrange("(q t r) -> t q r", t=PACK, r=RUN),
+                )
+            w1_rows = const.tile([P, PACK, D], BF16)
+            nc.sync.dma_start(out=w1_rows[:], in_=W1.rearrange("(c p) k -> p c k", p=P))
+            load_attn(2, whole)
+            for b in range(3, BATCHES):
+                load_x(b, whole)
+                load_attn(b, whole)
 
         warm = const.tile([P, 1], F32)
         nc.vector.memset(warm[:], 0.0)
@@ -382,13 +383,13 @@ def tile_block_pb_t_kernel(tc, attn_out, x, W_proj, b_proj, g2, beta2, W1, b1, o
             )
 
         def scalars_tokens(g):
-            return slice(width(g) - P * (GROUPS[g][2] // BATCH_TILES), width(g))
+            return slice(width(g) - (P * (GROUPS[g][2] // BATCH_TILES) if g < 7 else 0), width(g))
 
         def regroup_on_scalar(g):
             if not exists(g):
                 return
             h_grouped[g] = pairs.tile([P, WIDEST, PACK], BF16, name="h_grouped", align_bytes=64)
-            if GROUPS[g][2] == BATCH_TILES:
+            if GROUPS[g][2] == BATCH_TILES and g < 7:
                 regroup(nc.scalar.copy, g, scalars_tokens(g))
 
         def regroup_h(g):

@@ -16,18 +16,11 @@ RUN = 8
 PACK = 4
 D = P * PACK
 TOKENS = 4 * 1024
-BATCH_TILES = 4
-BATCHES = TOKENS // (BATCH_TILES * P)
-WIDEST = BATCH_TILES * P
-STAT_COLS = BATCHES * BATCH_TILES
+TILES = 4
+WIDTH = TILES * P
+GROUPS = TOKENS // WIDTH
+LAST = GROUPS - 1
 LN_EPS = 1e-6
-
-SMALL = BATCH_TILES // 2
-GROUPS = (
-    [(0, 0, 2), (0, 2, 2)]
-    + [(b, 0, BATCH_TILES) for b in range(1, BATCHES - 1)]
-    + [(BATCHES - 1, 0, 4)]
-)
 
 FLOPS = 2 * 2 * TOKENS * D * D
 
@@ -35,68 +28,74 @@ FLOPS = 2 * 2 * TOKENS * D * D
 def tile_block_pb_t_kernel(tc, attn_out, x, W_proj, b_proj, g2, beta2, W1, b1, out_0, out_1):
     nc = tc.nc
 
-    def by_batch(rows):
-        return rows.flatten_outer_dims().rearrange("(b p j) d -> b p j d", p=P, j=BATCH_TILES)
+    def by_group(rows):
+        return rows.flatten_outer_dims().rearrange("(g p j) d -> g p j d", p=P, j=TILES)
 
-    attn_batches, x_batches = by_batch(attn_out), by_batch(x)
-    x_mid_batches, u_batches = by_batch(out_0), by_batch(out_1)
+    attn_groups, x_groups = by_group(attn_out), by_group(x)
+    x_mid_groups, u_groups = by_group(out_0), by_group(out_1)
 
     with ExitStack() as ctx:
         const = ctx.enter_context(tc.tile_pool(name="const", bufs=1))
-        inputs = ctx.enter_context(tc.tile_pool(name="inputs", bufs=BATCHES))
+        inputs = ctx.enter_context(tc.tile_pool(name="inputs", bufs=GROUPS))
         pairs = ctx.enter_context(tc.tile_pool(name="pairs", bufs=2))
         triples = ctx.enter_context(tc.tile_pool(name="triples", bufs=3))
         sixes = ctx.enter_context(tc.tile_pool(name="sixes", bufs=6))
         flipped = ctx.enter_context(tc.psum_pool(name="flipped", bufs=4))
         sums = ctx.enter_context(tc.psum_pool(name="sums", bufs=4))
 
-        attn_rows, x_rows = {}, {}
-
-        def load_attn(b, tiles):
-            nc.sync.dma_start(out=attn_rows[b][:, tiles, :], in_=attn_batches[b][:, tiles, :])
-
-        def load_x(b, tiles):
-            nc.sync.dma_start(out=x_rows[b][:, tiles, :], in_=x_batches[b][:, tiles, :])
-
-        for b in range(BATCHES):
-            attn_rows[b] = inputs.tile([P, BATCH_TILES, D], BF16, name="attn_rows")
-            x_rows[b] = inputs.tile([P, BATCH_TILES, D], BF16, name="x_rows")
-
-        early = slice(0, SMALL)
-        late = slice(SMALL, BATCH_TILES)
-        whole = slice(0, BATCH_TILES)
         bias_rows = const.tile([P, 2, D], BF16)
         nc.gpsimd.memset(bias_rows[:, 0, :], 0.0)
         ones = const.tile([P, P], BF16)
         nc.vector.memset(ones[:], 1.0)
         ident_f32 = const.tile([P, P], F32)
         make_identity(nc, ident_f32[:])
+
+        attn_rows, x_rows = {}, {}
+        for g in range(GROUPS):
+            attn_rows[g] = inputs.tile([P, TILES, D], BF16, name="attn_rows")
+            x_rows[g] = inputs.tile([P, TILES, D], BF16, name="x_rows")
+        wp_rows = const.tile([P, PACK, D], BF16)
+        w1_rows = const.tile([P, PACK, D], BF16)
+        ln_rows = const.tile([P, P], BF16)
+
+        ALL = slice(0, TILES)
+        HALVES = (slice(0, TILES // 2), slice(TILES // 2, TILES))
+
+        def load_attn(g, tiles):
+            nc.sync.dma_start(out=attn_rows[g][:, tiles, :], in_=attn_groups[g][:, tiles, :])
+
+        def load_x(g, tiles):
+            nc.sync.dma_start(out=x_rows[g][:, tiles, :], in_=x_groups[g][:, tiles, :])
+
+        def load_weight(rows, weight):
+            nc.sync.dma_start(out=rows[:], in_=weight.rearrange("(c p) k -> p c k", p=P))
+
+        def load_bias(i, vec):
+            nc.sync.dma_start(out=bias_rows[0:1, i, :], in_=vec.rearrange("(o d) -> o d", o=1))
+
         with tc.manual_schedule(engines={mybir.EngineType.SP}):
-            load_x(0, early)
-            nc.sync.dma_start(out=bias_rows[0:1, 0, :], in_=b_proj.rearrange("(o d) -> o d", o=1))
-            wp_rows = const.tile([P, PACK, D], BF16)
-            nc.sync.dma_start(out=wp_rows[:], in_=W_proj.rearrange("(c p) k -> p c k", p=P))
-            load_x(0, late)
-            load_attn(0, early)
-            load_attn(0, late)
-            load_x(1, whole)
-            load_attn(1, whole)
-            load_x(2, whole)
+            load_x(0, HALVES[0])
+            load_bias(0, b_proj)
+            load_weight(wp_rows, W_proj)
+            load_attn(0, HALVES[0])
+            load_x(0, HALVES[1])
+            load_attn(0, HALVES[1])
+            load_x(1, ALL)
+            load_attn(1, ALL)
+            load_x(2, ALL)
             nc.vector.memset(bias_rows[:, 1, :], 0.0)
-            ln_rows = const.tile([P, P], BF16)
             nc.vector.memset(ln_rows[:], 0.0)
-            nc.sync.dma_start(out=bias_rows[0:1, 1, :], in_=b1.rearrange("(o d) -> o d", o=1))
+            load_bias(1, b1)
             for i, vec in enumerate((g2, beta2)):
                 nc.sync.dma_start(
                     out=ln_rows[i * PACK : (i + 1) * PACK, :].rearrange("t (q r) -> t q r", r=RUN),
                     in_=vec.rearrange("(q t r) -> t q r", t=PACK, r=RUN),
                 )
-            w1_rows = const.tile([P, PACK, D], BF16)
-            nc.sync.dma_start(out=w1_rows[:], in_=W1.rearrange("(c p) k -> p c k", p=P))
-            load_attn(2, whole)
-            for b in range(3, BATCHES):
-                load_x(b, whole)
-                load_attn(b, whole)
+            load_weight(w1_rows, W1)
+            load_attn(2, ALL)
+            for g in range(3, GROUPS):
+                load_x(g, ALL)
+                load_attn(g, ALL)
 
         warm = const.tile([P, 1], F32)
         nc.vector.memset(warm[:], 0.0)
@@ -104,67 +103,48 @@ def tile_block_pb_t_kernel(tc, attn_out, x, W_proj, b_proj, g2, beta2, W1, b1, o
 
         ident_bf16 = const.tile([P, P], BF16)
         make_identity(nc, ident_bf16[:])
-        neg_half = const.tile([P, BATCH_TILES], F32)
+        neg_half = const.tile([P, TILES], F32)
         nc.vector.memset(neg_half[:], -0.5)
 
-        row_sum = const.tile([P, STAT_COLS], F32)
-        neg_mean = const.tile([P, STAT_COLS], F32)
-        sq_sum = const.tile([P, STAT_COLS], F32)
-        var_eps = const.tile([P, STAT_COLS], F32)
-        rstd = const.tile([P, STAT_COLS], F32)
-
-        def width(g):
-            return GROUPS[g][2] * P
-
-        def tiles_of(g):
-            return range(GROUPS[g][2])
-
-        def batch_tiles(g):
-            b, first, count = GROUPS[g]
-            return b, slice(first, first + count)
+        row_sum = const.tile([P, GROUPS * TILES], F32)
+        neg_mean = const.tile([P, GROUPS * TILES], F32)
+        sq_sum = const.tile([P, GROUPS * TILES], F32)
+        var_eps = const.tile([P, GROUPS * TILES], F32)
+        rstd = const.tile([P, GROUPS * TILES], F32)
 
         def stat_cols(g):
-            b, first, count = GROUPS[g]
-            return slice(b * BATCH_TILES + first, b * BATCH_TILES + first + count)
+            return slice(g * TILES, (g + 1) * TILES)
 
         def stat_col(g, j):
-            b, first, count = GROUPS[g]
-            return slice(b * BATCH_TILES + first + j, b * BATCH_TILES + first + j + 1)
+            return slice(g * TILES + j, g * TILES + j + 1)
+
+        def exists(g):
+            return 0 <= g < GROUPS
 
         def flip_words(rows):
             row_words = rows.bitcast(F32)
-            banks = []
-            for half in range(rows.shape[1] // 2):
-                bank = flipped.tile([P, 2, 2 * P], F32, name="bank")
-                for jj in range(2):
-                    for u in range(2):
-                        nc.tensor.transpose(
-                            bank[:, u, jj * P : (jj + 1) * P],
-                            row_words[:, 2 * half + jj, u : 2 * P : 2],
-                            ident_f32[:],
-                        )
-                banks.append(bank)
-            return banks
+            bank = flipped.tile([P, 2, 2 * P], F32, name="bank")
+            for jj in range(2):
+                for u in range(2):
+                    nc.tensor.transpose(
+                        bank[:, u, jj * P : (jj + 1) * P], row_words[:, jj, u : 2 * P : 2], ident_f32[:]
+                    )
+            return bank
 
-        def copy_words(banks, grouped):
-            grouped_words = grouped.bitcast(F32)
-            for half, bank in enumerate(banks):
-                nc.scalar.copy(
-                    out=grouped_words[:, half * 2 * P : (half + 1) * 2 * P, :],
-                    in_=bank[:].rearrange("p u w -> p w u"),
-                )
+        def copy_words(bank, grouped):
+            nc.scalar.copy(out=grouped.bitcast(F32), in_=bank[:].rearrange("p u w -> p w u"))
 
-        def quantise(grouped, operand, start, stop):
+        def quantise(grouped, operand, cols):
             codes, scales = operand
             nc.vector.quantize_mx(
-                out=codes[:, start:stop].bitcast(FP8X4),
-                scales=scales[:, start:stop],
-                in_=grouped[:, start:stop, :].rearrange("p w t -> p (w t)"),
+                out=codes[:, cols].bitcast(FP8X4),
+                scales=scales[:, cols],
+                in_=grouped[:, cols, :].rearrange("p w t -> p (w t)"),
             )
 
         def mx_operand(pool, name):
-            codes = pool.tile([P, WIDEST], U32, name=name + "_codes", align_bytes=64)
-            scales = pool.tile([P, WIDEST], U8, name=name + "_scales", align_bytes=64)
+            codes = pool.tile([P, WIDTH], U32, name=name + "_codes", align_bytes=64)
+            scales = pool.tile([P, WIDTH], U8, name=name + "_scales", align_bytes=64)
             return codes, scales
 
         def matmul_mx_tile(acc, tokens_operand, j, weight_operand):
@@ -179,19 +159,19 @@ def tile_block_pb_t_kernel(tc, attn_out, x, W_proj, b_proj, g2, beta2, W1, b1, o
                 stop=True,
             )
 
+        def columns(tiles):
+            return slice(tiles.start * P, tiles.stop * P)
+
         b_proj_bcast = const.tile([P, 1, D], F32)
-        b1_bcast = const.tile([P, D], F32)
+        b1_bcast = const.tile([P, 1, D], F32)
         ln_cols = const.tile([P, 2 * PACK], F32)
 
-        def spread_b_proj():
+        def spread_bias(i):
             spread = sums.tile([P, 1, D], F32, name="acc")
-            nc.tensor.matmul(out=spread[:, 0, :], lhsT=ones[:], rhs=bias_rows[:, 0, :], start=True, stop=True)
+            nc.tensor.matmul(out=spread[:, 0, :], lhsT=ones[:], rhs=bias_rows[:, i, :], start=True, stop=True)
             return spread
 
-        def spread_b1_and_ln():
-            spread = sums.tile([P, D], F32, name="acc")
-            nc.tensor.matmul(out=spread[:], lhsT=ones[:], rhs=bias_rows[:, 1, :], start=True, stop=True)
-            nc.vector.tensor_copy(out=b1_bcast[:], in_=spread[:])
+        def spread_ln():
             ln_flipped = flipped.tile([P, P], BF16, name="bank")
             nc.tensor.transpose(ln_flipped[:], ln_rows[:], ident_bf16[:])
             nc.scalar.copy(out=ln_cols[:], in_=ln_flipped[:, 0 : 2 * PACK])
@@ -223,74 +203,54 @@ def tile_block_pb_t_kernel(tc, attn_out, x, W_proj, b_proj, g2, beta2, W1, b1, o
                     in_=bank[:].rearrange("p t n -> p n t"),
                 )
 
-        last = len(GROUPS) - 1
         a_banks, a_grouped, a_operand, a_sums = {}, {}, {}, {}
-        x_mid, h_sums = {}, {}
-        normed, h_banks, h_planes, h_grouped, h_operand, hidden = {}, {}, {}, {}, {}, {}
+        x_mid, normed, h_banks, h_planes = {}, {}, {}, {}
+        h_grouped, h_operand, h_sums, hidden = {}, {}, {}, {}
+
+        def flip_attention(g, halves=HALVES):
+            if exists(g):
+                for half in halves:
+                    a_banks[g, half.start] = flip_words(attn_rows[g][:, half, :])
+
+        def copy_attention(g, halves=HALVES):
+            if not exists(g):
+                return
+            if halves[0].start == 0:
+                a_grouped[g] = triples.tile([P, WIDTH, PACK], BF16, name="a_grouped", align_bytes=64)
+                a_operand[g] = mx_operand(triples, "a")
+            for half in halves:
+                copy_words(a_banks[g, half.start], a_grouped[g][:, columns(half), :])
+
+        def quantise_attention(g, tiles=ALL):
+            if exists(g):
+                quantise(a_grouped[g], a_operand[g], columns(tiles))
 
         def make_x_mid(g):
             if exists(g):
-                x_mid[g] = sixes.tile([P, BATCH_TILES, D], F32, name="x_mid")
+                x_mid[g] = sixes.tile([P, TILES, D], F32, name="x_mid")
 
-        def exists(g):
-            return 0 <= g < len(GROUPS)
+        def add_bias(engine, g, tiles, bias=b_proj_bcast):
+            if exists(g) and tiles.stop > tiles.start:
+                engine.tensor_tensor(
+                    out=x_mid[g][:, tiles, :],
+                    in0=x_rows[g][:, tiles, :],
+                    in1=bias[:].to_broadcast([P, tiles.stop - tiles.start, D]),
+                    op=ALU.add,
+                )
 
-        def flip_attention(g):
-            if not exists(g):
-                return
-            b, tiles = batch_tiles(g)
-            a_banks[g] = flip_words(attn_rows[b][:, tiles, :])
-
-        def copy_attention(g):
-            if not exists(g):
-                return
-            a_grouped[g] = triples.tile([P, WIDEST, PACK], BF16, name="a_grouped", align_bytes=64)
-            copy_words(a_banks[g], a_grouped[g][:])
-
-        def quantise_attention(g):
-            if not exists(g):
-                return
-            a_operand[g] = mx_operand(triples, "a")
-            quantise(a_grouped[g], a_operand[g], 0, width(g))
-
-        def add_bias(g, tiles, bias=b_proj_bcast):
-            if not exists(g) or len(tiles) == 0:
-                return
-            b, first, count = GROUPS[g]
-            nc.vector.tensor_tensor(
-                out=x_mid[g][:, tiles.start : tiles.stop, :],
-                in0=x_rows[b][:, first + tiles.start : first + tiles.stop, :],
-                in1=bias[:].to_broadcast([P, len(tiles), D]),
-                op=ALU.add,
-            )
-
-        def add_bias_on_gpsimd(g, tiles):
-            if not exists(g) or len(tiles) == 0:
-                return
-            b, first, count = GROUPS[g]
-            nc.gpsimd.tensor_tensor(
-                out=x_mid[g][:, tiles.start : tiles.stop, :],
-                in0=x_rows[b][:, first + tiles.start : first + tiles.stop, :],
-                in1=b_proj_bcast[:].to_broadcast([P, len(tiles), D]),
-                op=ALU.add,
-            )
-
-        def project_attention(g):
-            if not exists(g):
-                return
-            a_sums[g] = []
-            for j in tiles_of(g):
-                acc = sums.tile([P, D], F32, name="acc")
-                matmul_mx_tile(acc, a_operand[g], j, wp_operand)
-                a_sums[g].append(acc)
+        def project_attention(g, tiles=ALL):
+            if exists(g):
+                for j in range(tiles.start, tiles.stop):
+                    a_sums[g, j] = sums.tile([P, D], F32, name="acc")
+                    matmul_mx_tile(a_sums[g, j], a_operand[g], j, wp_operand)
 
         def add_attention(g):
             if not exists(g):
                 return
-            for j in tiles_of(g):
+            for j in range(TILES):
                 nc.vector.scalar_tensor_tensor(
                     out=x_mid[g][:, j, :],
-                    in0=a_sums[g][j][:],
+                    in0=a_sums[g, j][:],
                     scalar=1.0,
                     in1=x_mid[g][:, j, :],
                     op0=ALU.mult,
@@ -301,8 +261,8 @@ def tile_block_pb_t_kernel(tc, attn_out, x, W_proj, b_proj, g2, beta2, W1, b1, o
         def variance(g):
             if not exists(g):
                 return
-            squares = pairs.tile([P, BATCH_TILES, D], BF16, name="squares")
-            for j in tiles_of(g):
+            squares = pairs.tile([P, TILES, D], BF16, name="squares")
+            for j in range(TILES):
                 nc.scalar.activation(
                     out=squares[:, j, :],
                     in_=x_mid[g][:, j, :],
@@ -312,10 +272,9 @@ def tile_block_pb_t_kernel(tc, attn_out, x, W_proj, b_proj, g2, beta2, W1, b1, o
                     accum_out=sq_sum[:, stat_col(g, j)],
                 )
             nc.scalar.mul(out=neg_mean[:, stat_cols(g)], in_=row_sum[:, stat_cols(g)], mul=-1.0 / D)
-            b, tiles = batch_tiles(g)
-            nc.sync.dma_start(out=x_mid_batches[b][:, tiles, :], in_=x_mid[g][:, 0 : GROUPS[g][2], :])
+            nc.sync.dma_start(out=x_mid_groups[g], in_=x_mid[g][:])
 
-        def add_eps(g):
+        def reciprocal_std(g):
             if not exists(g):
                 return
             nc.vector.tensor_scalar(
@@ -326,22 +285,15 @@ def tile_block_pb_t_kernel(tc, attn_out, x, W_proj, b_proj, g2, beta2, W1, b1, o
                 op0=ALU.mult,
                 op1=ALU.add,
             )
-
-        def reciprocal_std(g):
-            if not exists(g):
-                return
             nc.gpsimd.tensor_tensor(
-                out=rstd[:, stat_cols(g)],
-                in0=var_eps[:, stat_cols(g)],
-                in1=neg_half[:, 0 : GROUPS[g][2]],
-                op=ALU.pow,
+                out=rstd[:, stat_cols(g)], in0=var_eps[:, stat_cols(g)], in1=neg_half[:], op=ALU.pow
             )
 
         def normalise(g):
             if not exists(g):
                 return
-            normed[g] = pairs.tile([P, BATCH_TILES, D], F32, name="normed")
-            for j in tiles_of(g):
+            normed[g] = pairs.tile([P, TILES, D], F32, name="normed")
+            for j in range(TILES):
                 nc.vector.tensor_scalar(
                     out=normed[g][:, j, :].rearrange("p (t q r) -> p t q r", t=PACK, r=RUN),
                     in0=x_mid[g][:, j, :].rearrange("p (q t r) -> p t q r", t=PACK, r=RUN),
@@ -354,147 +306,139 @@ def tile_block_pb_t_kernel(tc, attn_out, x, W_proj, b_proj, g2, beta2, W1, b1, o
         def flip_normed(g):
             if not exists(g):
                 return
-            h_banks[g] = []
             for t in range(PACK):
-                bank = flipped.tile([P, WIDEST], F32, name="bank")
-                for j in tiles_of(g):
+                h_banks[g, t] = flipped.tile([P, WIDTH], F32, name="bank")
+                for j in range(TILES):
                     nc.tensor.transpose(
-                        bank[:, j * P : (j + 1) * P], normed[g][:, j, t * P : (t + 1) * P], ident_f32[:]
+                        h_banks[g, t][:, j * P : (j + 1) * P], normed[g][:, j, t * P : (t + 1) * P], ident_f32[:]
                     )
-                h_banks[g].append(bank)
 
         def scale_shift(g):
             if not exists(g):
                 return
-            h_planes[g] = pairs.tile([P, PACK, WIDEST], BF16, name="h_planes")
+            h_planes[g] = pairs.tile([P, PACK, WIDTH], BF16, name="h_planes")
+            h_grouped[g] = pairs.tile([P, WIDTH, PACK], BF16, name="h_grouped", align_bytes=64)
             for t in range(PACK):
                 nc.scalar.activation(
-                    out=h_planes[g][:, t, 0 : width(g)],
-                    in_=h_banks[g][t][:, 0 : width(g)],
+                    out=h_planes[g][:, t, :],
+                    in_=h_banks[g, t][:],
                     func=ACT.Identity,
                     scale=ln_cols[:, t : t + 1],
                     bias=ln_cols[:, PACK + t : PACK + t + 1],
                 )
 
-        def regroup(copy, g, tokens):
-            copy(
-                out=h_grouped[g][:, tokens, :].rearrange("p (c i) t -> p c t i", i=4),
-                in_=h_planes[g][:, :, tokens].rearrange("p t (c i) -> p c t i", i=4),
-            )
+        def regroup(copy, g, tiles):
+            if exists(g) and tiles.stop > tiles.start:
+                copy(
+                    out=h_grouped[g][:, columns(tiles), :].rearrange("p (c i) t -> p c t i", i=4),
+                    in_=h_planes[g][:, :, columns(tiles)].rearrange("p t (c i) -> p c t i", i=4),
+                )
 
-        def scalars_tokens(g):
-            return slice(width(g) - (P * (GROUPS[g][2] // BATCH_TILES) if g < 7 else 0), width(g))
-
-        def regroup_on_scalar(g):
-            if not exists(g):
-                return
-            h_grouped[g] = pairs.tile([P, WIDEST, PACK], BF16, name="h_grouped", align_bytes=64)
-            if GROUPS[g][2] == BATCH_TILES and g < 7:
-                regroup(nc.scalar.copy, g, scalars_tokens(g))
-
-        def regroup_h(g):
+        def quantise_h(g, tiles):
             if exists(g):
-                mine = scalars_tokens(g).start
-                cuts = (0, width(g) // 2, mine) if g > last - 3 else (0, mine)
-                for start, stop in zip(cuts, cuts[1:]):
-                    regroup(nc.vector.tensor_copy, g, slice(start, stop))
-
-        def quantise_h(g):
-            if not exists(g):
-                return
-            h_operand[g] = mx_operand(pairs, "h")
-            cuts = (0, width(g) // 2, width(g)) if g > last - 3 else (0, width(g))
-            for start, stop in zip(cuts, cuts[1:]):
-                quantise(h_grouped[g], h_operand[g], start, stop)
+                if tiles.start == 0:
+                    h_operand[g] = mx_operand(pairs, "h")
+                quantise(h_grouped[g], h_operand[g], columns(tiles))
 
         def project_h(g):
-            if not exists(g):
-                return
-            for j in tiles_of(g):
-                h_sums[g, j] = sums.tile([P, D], F32, name="acc")
-                matmul_mx_tile(h_sums[g, j], h_operand[g], j, w1_operand)
+            if exists(g):
+                for j in range(TILES):
+                    h_sums[g, j] = sums.tile([P, D], F32, name="acc")
+                    matmul_mx_tile(h_sums[g, j], h_operand[g], j, w1_operand)
 
         def add_b1(g):
             if not exists(g):
                 return
-            hidden[g] = triples.tile([P, BATCH_TILES, D], F32, name="hidden")
-            for j in tiles_of(g):
-                nc.vector.tensor_tensor(out=hidden[g][:, j, :], in0=h_sums[g, j][:], in1=b1_bcast[:], op=ALU.add)
+            hidden[g] = triples.tile([P, TILES, D], F32, name="hidden")
+            for j in range(TILES):
+                nc.vector.tensor_tensor(
+                    out=hidden[g][:, j, :], in0=h_sums[g, j][:], in1=b1_bcast[:, 0, :], op=ALU.add
+                )
 
         def gelu(g):
             if not exists(g):
                 return
-            b, tiles = batch_tiles(g)
-            for j in tiles_of(g):
+            for j in range(TILES):
                 nc.scalar.activation(out=hidden[g][:, j, :], in_=hidden[g][:, j, :], func=ACT.Gelu)
-                nc.sync.dma_start(out=u_batches[b][:, tiles.start + j, :], in_=hidden[g][:, j, :])
+                nc.sync.dma_start(out=u_groups[g][:, j, :], in_=hidden[g][:, j, :])
 
-        def share(g):
-            return 0 if g < 4 or not exists(g) else 2 if g < 7 else 3
+        def on_gpsimd(g):
+            return (0, 4, 0, 1, 1)[g] if g < 5 else 3
 
         with tc.manual_schedule():
-            for g in range(4):
+            for g in range(3):
                 make_x_mid(g)
-            spread = spread_b_proj()
-            wp_grouped = triples.tile([P, WIDEST, PACK], BF16, name="a_grouped", align_bytes=64)
-            wp_banks = flip_words(wp_rows[:])
-            copy_words(wp_banks, wp_grouped[:])
-            flip_attention(0)
-            copy_attention(0)
-            flip_attention(1)
-            copy_attention(1)
-            add_bias(0, tiles_of(0), spread)
-            add_bias(1, tiles_of(1), spread)
-            nc.vector.tensor_copy(out=b_proj_bcast[:], in_=spread[:])
-            quantise(wp_grouped, wp_operand, 0, D)
-            quantise_attention(0)
-            project_attention(0)
-            add_bias(2, tiles_of(2), spread)
-            quantise_attention(1)
-            for step in range(len(GROUPS) + 3):
-                if step <= last:
+            b_proj_spread = spread_bias(0)
+            wp_grouped = triples.tile([P, WIDTH, PACK], BF16, name="a_grouped", align_bytes=64)
+            for half in HALVES:
+                copy_words(flip_words(wp_rows[:, half, :]), wp_grouped[:, columns(half), :])
+            for half in HALVES:
+                flip_attention(0, (half,))
+                copy_attention(0, (half,))
+                add_bias(nc.vector, 0, half, b_proj_spread)
+            nc.scalar.copy(out=b_proj_bcast[:], in_=b_proj_spread[:])
+            quantise(wp_grouped, wp_operand, columns(ALL))
+            for half in HALVES:
+                quantise_attention(0, half)
+                project_attention(0, half)
+            add_bias(nc.gpsimd, 1, ALL)
+            for step in range(GROUPS + 3):
+                ending = step >= LAST
+                if step <= LAST:
                     scale_shift(step - 2)
                 add_attention(step)
-                make_x_mid(step + 4)
+                make_x_mid(step + 3)
+                if step == 0:
+                    variance(0)
+                    flip_attention(1)
+                    copy_attention(1)
                 flip_attention(step + 2)
                 copy_attention(step + 2)
-                if step <= last:
-                    regroup_on_scalar(step - 2)
-                variance(step)
+                scalars = slice(TILES - 1, TILES) if 1 < step - 2 < LAST - 2 else slice(TILES, TILES)
+                if step <= LAST:
+                    regroup(nc.scalar.copy, step - 2, scalars)
+                if step > 0:
+                    variance(step)
+
                 if step == 0:
                     order_w1()
                 project_h(step - 3)
-                if step < last:
+                if not ending:
                     add_b1(step - 3)
-                add_bias_on_gpsimd(step + 2, range(share(step + 2)))
+                mine = slice(on_gpsimd(step + 2), TILES) if exists(step + 2) else ALL
+                add_bias(nc.gpsimd, step + 2, slice(0, mine.start))
+                if step <= 2:
+                    add_bias(nc.vector, step + 2, mine, b_proj_spread if step < 1 else b_proj_bcast)
                 if step == 1:
                     flip_w1()
-                if step == 0:
-                    spread_b1_and_ln()
-                if step < last:
-                    gelu(step - 3)
                 if step == 1:
-                    add_bias(3, tiles_of(3), spread)
-                if step == 2:
-                    add_bias(4, range(share(4), GROUPS[4][2]), spread)
+                    spread_ln()
+                if step == 1:
+                    b1_spread = spread_bias(1)
+                    nc.vector.tensor_copy(out=b1_bcast[:], in_=b1_spread[:])
+                if not ending:
+                    gelu(step - 3)
                 normalise(step - 1)
+                if step == 0:
+                    quantise_attention(1)
                 project_attention(step + 1)
                 flip_normed(step - 1)
-                if step >= last:
+                if ending:
                     scale_shift(step - 1)
-                    regroup_on_scalar(step - 1)
-                regroup_h(step - 2)
+                    regroup(nc.scalar.copy, step - 1, slice(TILES - 1, TILES) if 1 < step - 1 < LAST - 2 else slice(TILES, TILES))
+                pieces = HALVES if ending else (ALL,)
+                for tiles in pieces:
+                    regroup(nc.vector.tensor_copy, step - 2, slice(tiles.start, min(tiles.stop, scalars.start)))
                 quantise_attention(step + 2)
                 if step == 2:
-                    quantise(w1_grouped, w1_operand, 0, D)
-                if 3 <= step and exists(step + 2):
-                    add_bias(step + 2, range(share(step + 2), GROUPS[step + 2][2]))
-                if step < last:
-                    add_eps(step)
+                    quantise(w1_grouped, w1_operand, columns(ALL))
+                if step > 2:
+                    add_bias(nc.vector, step + 2, mine)
+                if not ending:
                     reciprocal_std(step)
-                quantise_h(step - 2)
-                if step >= last:
-                    add_eps(step)
+                for tiles in pieces:
+                    quantise_h(step - 2, tiles)
+                if ending:
                     reciprocal_std(step)
                     add_b1(step - 3)
                     gelu(step - 3)

@@ -49,6 +49,7 @@ def tile_block_pb_t_kernel(tc, attn_out, x, W_proj, b_proj, g2, beta2, W1, b1, o
         nc.vector.memset(ones[:], 1.0)
         ident_f32 = const.tile([P, P], F32)
         make_identity(nc, ident_f32[:])
+        nc.vector.memset(bias_rows[:, 1, :], 0.0)
 
         attn_rows, x_rows = {}, {}
         for g in range(GROUPS):
@@ -81,11 +82,10 @@ def tile_block_pb_t_kernel(tc, attn_out, x, W_proj, b_proj, g2, beta2, W1, b1, o
             load_x(0, HALVES[1])
             load_attn(0, HALVES[1])
             load_x(1, ALL)
+            load_bias(1, b1)
             load_attn(1, ALL)
             load_x(2, ALL)
-            nc.vector.memset(bias_rows[:, 1, :], 0.0)
             nc.vector.memset(ln_rows[:], 0.0)
-            load_bias(1, b1)
             for i, vec in enumerate((g2, beta2)):
                 nc.sync.dma_start(
                     out=ln_rows[i * PACK : (i + 1) * PACK, :].rearrange("t (q r) -> t q r", r=RUN),
@@ -377,6 +377,8 @@ def tile_block_pb_t_kernel(tc, attn_out, x, W_proj, b_proj, g2, beta2, W1, b1, o
                 copy_attention(0, (half,))
                 add_bias(nc.vector, 0, half, b_proj_spread)
             nc.scalar.copy(out=b_proj_bcast[:], in_=b_proj_spread[:])
+            b1_spread = spread_bias(1)
+            nc.scalar.copy(out=b1_bcast[:], in_=b1_spread[:])
             quantise(wp_grouped, wp_operand, columns(ALL))
             for half in HALVES:
                 quantise_attention(0, half)
@@ -413,9 +415,6 @@ def tile_block_pb_t_kernel(tc, attn_out, x, W_proj, b_proj, g2, beta2, W1, b1, o
                     flip_w1()
                 if step == 1:
                     spread_ln()
-                if step == 1:
-                    b1_spread = spread_bias(1)
-                    nc.vector.tensor_copy(out=b1_bcast[:], in_=b1_spread[:])
                 if not ending:
                     gelu(step - 3)
                 normalise(step - 1)

from contextlib import ExitStack

import concourse.mybir as mybir
from concourse.masks import make_identity

F32 = mybir.dt.float32
BF16 = mybir.dt.bfloat16
U32 = mybir.dt.uint32
U8 = mybir.dt.uint8
FP8X4 = mybir.dt.float8_e4m3fn_x4
ALU = mybir.AluOpType
ACT = mybir.ActivationFunctionType

P = 128
RUN = 8
PACK = 4
D = P * PACK
TOKENS = 4 * 1024
TILES = 4
WIDTH = TILES * P
GROUPS = TOKENS // WIDTH
LAST = GROUPS - 1
LN_EPS = 1e-6

FLOPS = 2 * 2 * TOKENS * D * D


def tile_block_pb_t_kernel(tc, attn_out, x, W_proj, b_proj, g2, beta2, W1, b1, out_0, out_1):
    nc = tc.nc

    def by_group(rows):
        return rows.flatten_outer_dims().rearrange("(g p j) d -> g p j d", p=P, j=TILES)

    attn_groups, x_groups = by_group(attn_out), by_group(x)
    x_mid_groups, u_groups = by_group(out_0), by_group(out_1)

    with ExitStack() as ctx:
        const = ctx.enter_context(tc.tile_pool(name="const", bufs=1))
        inputs = ctx.enter_context(tc.tile_pool(name="inputs", bufs=GROUPS))
        pairs = ctx.enter_context(tc.tile_pool(name="pairs", bufs=2))
        triples = ctx.enter_context(tc.tile_pool(name="triples", bufs=3))
        sixes = ctx.enter_context(tc.tile_pool(name="sixes", bufs=6))
        flipped = ctx.enter_context(tc.psum_pool(name="flipped", bufs=4))
        sums = ctx.enter_context(tc.psum_pool(name="sums", bufs=4))

        bias_rows = const.tile([P, 2, D], BF16)
        nc.gpsimd.memset(bias_rows[:, 0, :], 0.0)
        ones = const.tile([P, P], BF16)
        nc.vector.memset(ones[:], 1.0)
        ident_f32 = const.tile([P, P], F32)
        make_identity(nc, ident_f32[:])
        nc.vector.memset(bias_rows[:, 1, :], 0.0)

        attn_rows, x_rows = {}, {}
        for g in range(GROUPS):
            attn_rows[g] = inputs.tile([P, TILES, D], BF16, name="attn_rows")
            x_rows[g] = inputs.tile([P, TILES, D], BF16, name="x_rows")
        wp_rows = const.tile([P, PACK, D], BF16)
        w1_rows = const.tile([P, PACK, D], BF16)
        ln_rows = const.tile([P, P], BF16)

        ALL = slice(0, TILES)
        HALVES = (slice(0, TILES // 2), slice(TILES // 2, TILES))

        def load_attn(g, tiles):
            nc.sync.dma_start(out=attn_rows[g][:, tiles, :], in_=attn_groups[g][:, tiles, :])

        def load_x(g, tiles):
            nc.sync.dma_start(out=x_rows[g][:, tiles, :], in_=x_groups[g][:, tiles, :])

        def load_weight(rows, weight):
            nc.sync.dma_start(out=rows[:], in_=weight.rearrange("(c p) k -> p c k", p=P))

        def load_bias(i, vec):
            nc.sync.dma_start(out=bias_rows[0:1, i, :], in_=vec.rearrange("(o d) -> o d", o=1))

        with tc.manual_schedule(engines={mybir.EngineType.SP}):
            load_x(0, HALVES[0])
            load_bias(0, b_proj)
            load_weight(wp_rows, W_proj)
            load_attn(0, HALVES[0])
            load_x(0, HALVES[1])
            load_attn(0, HALVES[1])
            load_x(1, ALL)
            load_bias(1, b1)
            load_attn(1, ALL)
            load_x(2, ALL)
            nc.vector.memset(ln_rows[:], 0.0)
            for i, vec in enumerate((g2, beta2)):
                nc.sync.dma_start(
                    out=ln_rows[i * PACK : (i + 1) * PACK, :].rearrange("t (q r) -> t q r", r=RUN),
                    in_=vec.rearrange("(q t r) -> t q r", t=PACK, r=RUN),
                )
            load_weight(w1_rows, W1)
            load_attn(2, ALL)
            for g in range(3, GROUPS):
                load_x(g, ALL)
                load_attn(g, ALL)

        warm = const.tile([P, 1], F32)
        nc.vector.memset(warm[:], 0.0)
        nc.scalar.activation(out=warm[:], in_=warm[:], func=ACT.Gelu)

        ident_bf16 = const.tile([P, P], BF16)
        make_identity(nc, ident_bf16[:])
        neg_half = const.tile([P, TILES], F32)
        nc.vector.memset(neg_half[:], -0.5)

        row_sum = const.tile([P, GROUPS * TILES], F32)
        neg_mean = const.tile([P, GROUPS * TILES], F32)
        sq_sum = const.tile([P, GROUPS * TILES], F32)
        var_eps = const.tile([P, GROUPS * TILES], F32)
        rstd = const.tile([P, GROUPS * TILES], F32)

        def stat_cols(g):
            return slice(g * TILES, (g + 1) * TILES)

        def stat_col(g, j):
            return slice(g * TILES + j, g * TILES + j + 1)

        def exists(g):
            return 0 <= g < GROUPS

        def flip_words(rows):
            row_words = rows.bitcast(F32)
            bank = flipped.tile([P, 2, 2 * P], F32, name="bank")
            for jj in range(2):
                for u in range(2):
                    nc.tensor.transpose(
                        bank[:, u, jj * P : (jj + 1) * P], row_words[:, jj, u : 2 * P : 2], ident_f32[:]
                    )
            return bank

        def copy_words(bank, grouped):
            nc.scalar.copy(out=grouped.bitcast(F32), in_=bank[:].rearrange("p u w -> p w u"))

        def quantise(grouped, operand, cols):
            codes, scales = operand
            nc.vector.quantize_mx(
                out=codes[:, cols].bitcast(FP8X4),
                scales=scales[:, cols],
                in_=grouped[:, cols, :].rearrange("p w t -> p (w t)"),
            )

        def mx_operand(pool, name):
            codes = pool.tile([P, WIDTH], U32, name=name + "_codes", align_bytes=64)
            scales = pool.tile([P, WIDTH], U8, name=name + "_scales", align_bytes=64)
            return codes, scales

        def matmul_mx_tile(acc, tokens_operand, j, weight_operand):
            tokens = slice(j * P, (j + 1) * P)
            nc.tensor.matmul_mx(
                out=acc[:],
                lhsT=tokens_operand[0][:, tokens].bitcast(FP8X4),
                lhsT_scale=tokens_operand[1][:, tokens],
                rhs=weight_operand[0][:].bitcast(FP8X4),
                rhs_scale=weight_operand[1][:],
                start=True,
                stop=True,
            )

        def columns(tiles):
            return slice(tiles.start * P, tiles.stop * P)

        b_proj_bcast = const.tile([P, 1, D], F32)
        b1_bcast = const.tile([P, 1, D], F32)
        ln_cols = const.tile([P, 2 * PACK], F32)

        def spread_bias(i):
            spread = sums.tile([P, 1, D], F32, name="acc")
            nc.tensor.matmul(out=spread[:, 0, :], lhsT=ones[:], rhs=bias_rows[:, i, :], start=True, stop=True)
            return spread

        def spread_ln():
            ln_flipped = flipped.tile([P, P], BF16, name="bank")
            nc.tensor.transpose(ln_flipped[:], ln_rows[:], ident_bf16[:])
            nc.scalar.copy(out=ln_cols[:], in_=ln_flipped[:, 0 : 2 * PACK])

        wp_operand = mx_operand(const, "wp")
        w1_operand = mx_operand(const, "w1")
        w1_grouped = const.tile([P, D, PACK], BF16, align_bytes=64)
        w1_ordered = const.tile([P, PACK, D], BF16)

        def order_w1():
            for c in range(PACK):
                nc.scalar.copy(
                    out=w1_ordered[:, c, :].rearrange("p (t q r) -> p t q r", t=PACK, r=RUN),
                    in_=w1_rows[:, c, :].rearrange("p (q t r) -> p t q r", t=PACK, r=RUN),
                )

        def flip_w1():
            for half in range(2):
                bank = flipped.tile([P, PACK, 2 * P], BF16, name="bank")
                for cc in range(2):
                    for t in range(PACK):
                        nc.tensor.transpose(
                            bank[:, t, cc * P : (cc + 1) * P],
                            w1_ordered[:, 2 * half + cc, t * P : (t + 1) * P],
                            ident_bf16[:],
                        )
                nc.scalar.copy(
                    out=w1_grouped[:, half * 2 * P : (half + 1) * 2 * P, :],
                    in_=bank[:].rearrange("p t n -> p n t"),
                )

        a_banks, a_grouped, a_operand, a_sums = {}, {}, {}, {}
        x_mid, normed, h_banks, h_planes = {}, {}, {}, {}
        h_grouped, h_operand, h_sums, hidden = {}, {}, {}, {}

        def flip_attention(g, halves=HALVES):
            if exists(g):
                for half in halves:
                    a_banks[g, half.start] = flip_words(attn_rows[g][:, half, :])

        def copy_attention(g, halves=HALVES):
            if not exists(g):
                return
            if halves[0].start == 0:
                a_grouped[g] = triples.tile([P, WIDTH, PACK], BF16, name="a_grouped", align_bytes=64)
                a_operand[g] = mx_operand(triples, "a")
            for half in halves:
                copy_words(a_banks[g, half.start], a_grouped[g][:, columns(half), :])

        def quantise_attention(g, tiles=ALL):
            if exists(g):
                quantise(a_grouped[g], a_operand[g], columns(tiles))

        def make_x_mid(g):
            if exists(g):
                x_mid[g] = sixes.tile([P, TILES, D], F32, name="x_mid")

        def add_bias(engine, g, tiles, bias=b_proj_bcast):
            if exists(g) and tiles.stop > tiles.start:
                engine.tensor_tensor(
                    out=x_mid[g][:, tiles, :],
                    in0=x_rows[g][:, tiles, :],
                    in1=bias[:].to_broadcast([P, tiles.stop - tiles.start, D]),
                    op=ALU.add,
                )

        def project_attention(g, tiles=ALL):
            if exists(g):
                for j in range(tiles.start, tiles.stop):
                    a_sums[g, j] = sums.tile([P, D], F32, name="acc")
                    matmul_mx_tile(a_sums[g, j], a_operand[g], j, wp_operand)

        def add_attention(g):
            if not exists(g):
                return
            for j in range(TILES):
                nc.vector.scalar_tensor_tensor(
                    out=x_mid[g][:, j, :],
                    in0=a_sums[g, j][:],
                    scalar=1.0,
                    in1=x_mid[g][:, j, :],
                    op0=ALU.mult,
                    op1=ALU.add,
                    accum_out=row_sum[:, stat_col(g, j)],
                )

        def variance(g):
            if not exists(g):
                return
            squares = pairs.tile([P, TILES, D], BF16, name="squares")
            for j in range(TILES):
                nc.scalar.activation(
                    out=squares[:, j, :],
                    in_=x_mid[g][:, j, :],
                    func=ACT.Square,
                    bias=row_sum[:, stat_col(g, j)],
                    scale=-float(D),
                    accum_out=sq_sum[:, stat_col(g, j)],
                )
            nc.scalar.mul(out=neg_mean[:, stat_cols(g)], in_=row_sum[:, stat_cols(g)], mul=-1.0 / D)
            nc.sync.dma_start(out=x_mid_groups[g], in_=x_mid[g][:])

        def reciprocal_std(g):
            if not exists(g):
                return
            nc.vector.tensor_scalar(
                out=var_eps[:, stat_cols(g)],
                in0=sq_sum[:, stat_cols(g)],
                scalar1=1.0 / D**3,
                scalar2=LN_EPS,
                op0=ALU.mult,
                op1=ALU.add,
            )
            nc.gpsimd.tensor_tensor(
                out=rstd[:, stat_cols(g)], in0=var_eps[:, stat_cols(g)], in1=neg_half[:], op=ALU.pow
            )

        def normalise(g):
            if not exists(g):
                return
            normed[g] = pairs.tile([P, TILES, D], F32, name="normed")
            for j in range(TILES):
                nc.vector.tensor_scalar(
                    out=normed[g][:, j, :].rearrange("p (t q r) -> p t q r", t=PACK, r=RUN),
                    in0=x_mid[g][:, j, :].rearrange("p (q t r) -> p t q r", t=PACK, r=RUN),
                    scalar1=neg_mean[:, stat_col(g, j)],
                    scalar2=rstd[:, stat_col(g, j)],
                    op0=ALU.add,
                    op1=ALU.mult,
                )

        def flip_normed(g):
            if not exists(g):
                return
            for t in range(PACK):
                h_banks[g, t] = flipped.tile([P, WIDTH], F32, name="bank")
                for j in range(TILES):
                    nc.tensor.transpose(
                        h_banks[g, t][:, j * P : (j + 1) * P], normed[g][:, j, t * P : (t + 1) * P], ident_f32[:]
                    )

        def scale_shift(g):
            if not exists(g):
                return
            h_planes[g] = pairs.tile([P, PACK, WIDTH], BF16, name="h_planes")
            h_grouped[g] = pairs.tile([P, WIDTH, PACK], BF16, name="h_grouped", align_bytes=64)
            for t in range(PACK):
                nc.scalar.activation(
                    out=h_planes[g][:, t, :],
                    in_=h_banks[g, t][:],
                    func=ACT.Identity,
                    scale=ln_cols[:, t : t + 1],
                    bias=ln_cols[:, PACK + t : PACK + t + 1],
                )

        def regroup(copy, g, tiles):
            if exists(g) and tiles.stop > tiles.start:
                copy(
                    out=h_grouped[g][:, columns(tiles), :].rearrange("p (c i) t -> p c t i", i=4),
                    in_=h_planes[g][:, :, columns(tiles)].rearrange("p t (c i) -> p c t i", i=4),
                )

        def quantise_h(g, tiles):
            if exists(g):
                if tiles.start == 0:
                    h_operand[g] = mx_operand(pairs, "h")
                quantise(h_grouped[g], h_operand[g], columns(tiles))

        def project_h(g):
            if exists(g):
                for j in range(TILES):
                    h_sums[g, j] = sums.tile([P, D], F32, name="acc")
                    matmul_mx_tile(h_sums[g, j], h_operand[g], j, w1_operand)

        def add_b1(g):
            if not exists(g):
                return
            hidden[g] = triples.tile([P, TILES, D], F32, name="hidden")
            for j in range(TILES):
                nc.vector.tensor_tensor(
                    out=hidden[g][:, j, :], in0=h_sums[g, j][:], in1=b1_bcast[:, 0, :], op=ALU.add
                )

        def gelu(g):
            if not exists(g):
                return
            for j in range(TILES):
                nc.scalar.activation(out=hidden[g][:, j, :], in_=hidden[g][:, j, :], func=ACT.Gelu)
                nc.sync.dma_start(out=u_groups[g][:, j, :], in_=hidden[g][:, j, :])

        def on_gpsimd(g):
            return (0, 4, 0, 1, 1)[g] if g < 5 else 3

        with tc.manual_schedule():
            for g in range(3):
                make_x_mid(g)
            b_proj_spread = spread_bias(0)
            wp_grouped = triples.tile([P, WIDTH, PACK], BF16, name="a_grouped", align_bytes=64)
            for half in HALVES:
                copy_words(flip_words(wp_rows[:, half, :]), wp_grouped[:, columns(half), :])
            for half in HALVES:
                flip_attention(0, (half,))
                copy_attention(0, (half,))
                add_bias(nc.vector, 0, half, b_proj_spread)
            nc.scalar.copy(out=b_proj_bcast[:], in_=b_proj_spread[:])
            b1_spread = spread_bias(1)
            nc.scalar.copy(out=b1_bcast[:], in_=b1_spread[:])
            quantise(wp_grouped, wp_operand, columns(ALL))
            for half in HALVES:
                quantise_attention(0, half)
                project_attention(0, half)
            add_bias(nc.gpsimd, 1, ALL)
            for step in range(GROUPS + 3):
                ending = step >= LAST
                if step <= LAST:
                    scale_shift(step - 2)
                add_attention(step)
                make_x_mid(step + 3)
                if step == 0:
                    variance(0)
                    flip_attention(1)
                    copy_attention(1)
                flip_attention(step + 2)
                copy_attention(step + 2)
                scalars = slice(TILES - 1, TILES) if 1 < step - 2 < LAST - 2 else slice(TILES, TILES)
                if step <= LAST:
                    regroup(nc.scalar.copy, step - 2, scalars)
                if step > 0:
                    variance(step)

                if step == 0:
                    order_w1()
                project_h(step - 3)
                if not ending:
                    add_b1(step - 3)
                mine = slice(on_gpsimd(step + 2), TILES) if exists(step + 2) else ALL
                add_bias(nc.gpsimd, step + 2, slice(0, mine.start))
                if step <= 2:
                    add_bias(nc.vector, step + 2, mine, b_proj_spread if step < 1 else b_proj_bcast)
                if step == 1:
                    flip_w1()
                if step == 1:
                    spread_ln()
                if not ending:
                    gelu(step - 3)
                normalise(step - 1)
                if step == 0:
                    quantise_attention(1)
                project_attention(step + 1)
                flip_normed(step - 1)
                if ending:
                    scale_shift(step - 1)
                    regroup(nc.scalar.copy, step - 1, slice(TILES - 1, TILES) if 1 < step - 1 < LAST - 2 else slice(TILES, TILES))
                pieces = HALVES if ending else (ALL,)
                for tiles in pieces:
                    regroup(nc.vector.tensor_copy, step - 2, slice(tiles.start, min(tiles.stop, scalars.start)))
                quantise_attention(step + 2)
                if step == 2:
                    quantise(w1_grouped, w1_operand, columns(ALL))
                if step > 2:
                    add_bias(nc.vector, step + 2, mine)
                if not ending:
                    reciprocal_std(step)
                for tiles in pieces:
                    quantise_h(step - 2, tiles)
                if ending:
                    reciprocal_std(step)
                    add_b1(step - 3)
                    gelu(step - 3)
